import numpy as np
import ml_dtypes


def mxq(x, axis, fmt="e4m3"):
    dtype, down = {"e4m3": (ml_dtypes.float8_e4m3fn, 7), "e5m2": (ml_dtypes.float8_e5m2, 14)}[fmt]
    v = np.moveaxis(np.asarray(x, np.float32).astype(ml_dtypes.bfloat16).astype(np.float64), axis, -1)
    blocks = v.reshape(v.shape[:-1] + (-1, 32))
    amax = np.abs(blocks).max(-1, keepdims=True)
    byte = np.maximum(np.where(amax > 0, np.frexp(amax)[1] - 1 + 127, 0) - down, 1)
    scale = np.exp2(byte - 127.0)
    codes = (blocks / scale).astype(np.float32).astype(dtype).astype(np.float64)
    return np.moveaxis((codes * scale).reshape(v.shape), -1, axis)


WIDE = False


def mx_kscale(k):
    if not WIDE:
        return np.ones(k)
    levels = np.array([10, -10, 5, -5, 0])
    a = np.random.permutation(np.resize(levels, k // 512 * 4)).reshape(k // 512, 4)
    idx = np.arange(k)
    return np.exp2(a[idx // 512, idx % 128 // 32])


BF16 = ml_dtypes.bfloat16


def bf(x):
    return np.asarray(x, np.float32).astype(BF16)


def f64(x):
    return np.asarray(x).astype(np.float64)


B, N, D, H, NS, SK1, SK2 = 1, 2048, 1024, 16, 10, 512, 1024
HD = D // H
D4 = np.array([0.4829629131445341, 0.8365163037378079, 0.2241438680420134, -0.1294095225512604])
TAPS = len(D4)
SPARSE_DILATIONS = (SK1, SK2)


def softmax(v, axis):
    e = np.exp(v - v.max(axis, keepdims=True))
    return e / e.sum(axis, keepdims=True)


def sigmoid(v):
    return 1.0 / (1.0 + np.exp(-v))


def shift_right(t, s):
    if s == 0:
        return t
    return np.pad(t, ((0, 0), (0, 0), (s, 0), (0, 0)))[:, :, :N, :]


def to_heads(t):
    return t.reshape(B, N, H, HD).transpose(0, 2, 1, 3)


def setup_inputs():
    s = mx_kscale(D)
    return {"x": bf(np.random.standard_normal((B, N, D)) * s),
            "Wkv": bf(np.random.standard_normal((D, D + D)) * D ** -0.5 / s[:, None]),
            "bkv": bf(np.random.standard_normal(D + D) * 0.2),
            "scale_gain": bf(np.random.standard_normal((NS, H)) * 0.5),
            "skip_w": bf(-1.0 + np.random.standard_normal(len(SPARSE_DILATIONS)) * 0.3)}


def reference(x, Wkv, bkv, scale_gain, skip_w):
    kv = (mxq(f64(x), 2, "e4m3") @ mxq(f64(Wkv), 0, "e4m3")) + f64(bkv)
    k, v = to_heads(kv[..., :D]), to_heads(kv[..., D:])
    k_mag = np.sqrt((k * k).sum(-1, keepdims=True))
    field = v * k_mag
    gains = softmax(f64(scale_gain), 0)
    acc = np.zeros_like(field)
    for j in range(NS):
        d = 1 << j
        y = sum(D4[t] * shift_right(field, (TAPS - 1 - t) * d) for t in range(TAPS))
        acc = acc + gains[j][None, :, None, None] * y
    field = acc
    sw = sigmoid(f64(skip_w))
    skip = sum(sw[i] * shift_right(field, d) for i, d in enumerate(SPARSE_DILATIONS))
    return field + skip

@@ -1,0 +1,439 @@
+from contextlib import ExitStack
+
+import concourse.mybir as mybir
+from concourse.masks import make_identity
+
+F32 = mybir.dt.float32
+BF16 = mybir.dt.bfloat16
+U32 = mybir.dt.uint32
+U8 = mybir.dt.uint8
+FP8X4 = mybir.dt.float8_e4m3fn_x4
+ALU = mybir.AluOpType
+ACT = mybir.ActivationFunctionType
+AX = mybir.AxisListType
+
+P = 128
+NTOK = 2048
+DM = 1024
+NH = 16
+HD = 64
+NB = 8
+NQ = 256
+HALO = 8
+D4 = (0.4829629131445341, 0.8365163037378079, 0.2241438680420134, -0.1294095225512604)
+FLOPS = 2 * NTOK * DM * 2 * DM
+
+FROW = NH * 384 + 1
+TOEP_BASE = 9 * NTOK * HD
+MAG_BASE = 15 * NTOK * HD + NTOK * HD // 2
+SMALL_TAPS = ((1, 0), (2, 1), (3, 3), (4, 2), (6, 4), (12, 5))
+
+
+def tile_causalwaveletfieldattentionh_pa_kernel(tc, x, Wkv, bkv, scale_gain, skip_w, out):
+    nc = tc.nc
+    d0, d1, d2, d3 = D4
+    oflat = out.rearrange("o h n c -> (o h n c)")
+    oview = out.rearrange("o h (t p b) c -> p (o h) t (b c)", t=2, p=P, b=NB)
+    xview = x.rearrange("o (t p b) k -> p (o t) b k", t=2, p=P, b=NB)
+
+    with ExitStack() as ctx:
+        const = ctx.enter_context(tc.tile_pool(name="const", bufs=1))
+        wst_pool = ctx.enter_context(tc.tile_pool(name="wst", bufs=2))
+        pre = ctx.enter_context(tc.tile_pool(name="pre", bufs=2))
+        main = ctx.enter_context(tc.tile_pool(name="main", bufs=2))
+        ps = ctx.enter_context(tc.psum_pool(name="ps", bufs=1))
+
+        ident = const.tile([P, P], F32, name="ident")
+        make_identity(nc, ident[:])
+        ind = const.tile([P, 2], F32, name="ind")
+        nc.vector.memset(ind[:], 0.0)
+        nc.vector.memset(ind[0:64, 0:1], 1.0)
+        nc.vector.memset(ind[64:128, 1:2], 1.0)
+        magt = const.tile([P, P], F32, name="magt")
+        nc.vector.memset(magt[:], 0.0)
+        bkf = const.tile([P, P], F32, name="bkf")
+        nc.vector.memset(bkf[:], 0.0)
+        fts = [const.tile([P, NB, HALO + NQ], F32, name="ft%d" % j) for j in range(2)]
+        for j in range(2):
+            nc.gpsimd.memset(fts[j][:, :, 0:HALO], 0.0)
+
+        xc = const.tile([P, 2, NTOK], U32, name="xc", align_bytes=64)
+        xsc = const.tile([P, 2, NTOK], U8, name="xsc", align_bytes=64)
+        wc = const.tile([P, 2, 2 * DM], U32, name="wc", align_bytes=64)
+        wsc = const.tile([P, 2, 2 * DM], U8, name="wsc", align_bytes=64)
+        wt = const.tile([P, NH, NQ], F32, name="wt")
+        bT = const.tile([P, 16], F32, name="bT")
+        csm = const.tile([P, 8, 6], F32, name="csm")
+        sw = const.tile([P, 2], F32, name="sw")
+
+        sgb = const.tile([P, 160], BF16, name="sgb")
+        nc.sync.dma_start(out=sgb[:], in_=scale_gain.rearrange("j h -> (j h)").partition_broadcast(P))
+        skb = const.tile([P, 2], BF16, name="skb")
+        nc.sync.dma_start(out=skb[:], in_=skip_w.partition_broadcast(P))
+        bkb = const.tile([16, P], BF16, name="bkb")
+        nc.sync.dma_start(out=bkb[:], in_=bkv.rearrange("(m c) -> m c", c=P))
+
+        def load_w(c0):
+            wst = wst_pool.tile([P, 2, 4, 512], BF16, name="wst")
+            for g in range(2):
+                for u in range(2):
+                    r0 = 512 * g + 256 * u
+                    nc.sync.dma_start(
+                        out=wst[:, g, 2 * u : 2 * u + 2, :],
+                        in_=Wkv[r0 : r0 + 256, c0 : c0 + 512].rearrange("(p e) c -> p e c", e=2),
+                    )
+            return wst
+
+        def quant_w(wst, c0, on_vector):
+            if on_vector:
+                wg = wst_pool.tile([P, 2, 512, 4], BF16, name="wg", bufs=1, align_bytes=64)
+            else:
+                wg = main.tile([P, 2, 512, 4], BF16, name="wg2", tag="ut", align_bytes=64)
+            for g in range(2):
+                if on_vector:
+                    nc.vector.tensor_copy(
+                        out=wg[:, g].rearrange("p (c i) t -> p c t i", i=4),
+                        in_=wst[:, g].rearrange("p t (c i) -> p c t i", i=4),
+                    )
+                else:
+                    nc.scalar.copy(out=wg[:, g], in_=wst[:, g].rearrange("p t c -> p c t"))
+            for g in range(2):
+                nc.vector.quantize_mx(
+                    out=wc[:, g, c0 : c0 + 512].bitcast(FP8X4),
+                    scales=wsc[:, g, c0 : c0 + 512],
+                    in_=wg[:, g].rearrange("p c t -> p (c t)"),
+                )
+
+        def load_x(be):
+            xs = pre.tile([P, 2, 2, DM], BF16, name="xs")
+            nc.sync.dma_start(out=xs[:], in_=xview[:, :, 2 * be : 2 * be + 2, :])
+            return xs
+
+        wst_a = load_w(0)
+        xss = {0: load_x(0), 1: load_x(1)}
+
+        nc.vector.tensor_copy(out=bkf[0:16, :], in_=bkb[:])
+        bps = ps.tile([P, P], F32, name="bps", tag="sm")
+        nc.tensor.transpose(bps[:], bkf[:], ident[:])
+        nc.vector.tensor_copy(out=bT[:], in_=bps[:, 0:16])
+
+        quant_w(wst_a, 0, True)
+
+        for be in range(4):
+            xs = xss[be]
+            xg = pre.tile([P, 2, 512, 4], BF16, name="xg", align_bytes=64)
+            xg32 = xg[:].bitcast(F32)
+            for g in range(2):
+                for bb in range(2):
+                    xt = ps.tile([P, 2, 2, P], F32, name="xt", tag=("tr" if bb == 0 else "ob"), bufs=(2 if bb == 0 else 3))
+                    for t in range(2):
+                        xw = xs[:, t, bb, :].bitcast(F32)
+                        for u in range(2):
+                            w0 = 256 * g + 128 * u
+                            nc.tensor.transpose(xt[:, t, u, :], xw[:, w0 : w0 + 128], ident[:])
+                    dst = xg32[:, g, 256 * bb : 256 * bb + 256, :].rearrange("p (t k) u -> p t k u", t=2)
+                    src = xt[:].rearrange("p t u k -> p t k u")
+                    if bb == 0:
+                        nc.vector.tensor_copy(out=dst, in_=src)
+                    else:
+                        nc.scalar.copy(out=dst, in_=src)
+            if be + 2 < 4:
+                xss[be + 2] = load_x(be + 2)
+            if be == 1:
+                wst_b = load_w(DM)
+                wst_c = load_w(512)
+            for g in range(2):
+                nc.vector.quantize_mx(
+                    out=xc[:, g, 512 * be : 512 * be + 512].bitcast(FP8X4),
+                    scales=xsc[:, g, 512 * be : 512 * be + 512],
+                    in_=xg[:, g].rearrange("p c j -> p (c j)"),
+                )
+
+        quant_w(wst_b, DM, True)
+        wst_d = load_w(DM + 512)
+
+        sg = const.tile([P, 10, NH], F32, name="sg")
+        nc.vector.tensor_copy(out=sg[:].rearrange("p j h -> p (j h)"), in_=sgb[:])
+        mxg = const.tile([P, NH], F32, name="mxg")
+        nc.vector.tensor_reduce(out=mxg[:], in_=sg[:].rearrange("p j h -> p h j"), axis=AX.X, op=ALU.max)
+        nc.vector.tensor_tensor(
+            out=sg[:], in0=sg[:], in1=mxg[:].unsqueeze(1).to_broadcast([P, 10, NH]), op=ALU.subtract
+        )
+        eg = const.tile([P, 10, NH], F32, name="eg")
+        nc.scalar.activation(out=eg[:], in_=sg[:], func=ACT.Exp)
+        ssum = const.tile([P, NH], F32, name="ssum")
+        nc.vector.tensor_reduce(out=ssum[:], in_=eg[:].rearrange("p j h -> p h j"), axis=AX.X, op=ALU.add)
+        rsum = const.tile([P, NH], F32, name="rsum")
+        nc.vector.reciprocal(out=rsum[:], in_=ssum[:])
+        gn = const.tile([P, 10, NH], F32, name="gn")
+        nc.vector.tensor_tensor(
+            out=gn[:], in0=eg[:], in1=rsum[:].unsqueeze(1).to_broadcast([P, 10, NH]), op=ALU.mult
+        )
+        pt = const.tile([P, 11, NH], F32, name="pt")
+        nc.vector.memset(pt[:, 10:11, :], 0.0)
+        nc.vector.tensor_scalar_mul(out=pt[:, 0:10, :], in0=gn[:], scalar1=d2)
+        nc.vector.scalar_tensor_tensor(
+            out=pt[:, 1:11, :], in0=gn[:], scalar=d1, in1=pt[:, 1:11, :], op0=ALU.mult, op1=ALU.add
+        )
+        rt = const.tile([P, 10, NH], F32, name="rt")
+        nc.vector.tensor_scalar_mul(out=rt[:], in0=gn[:], scalar1=d0)
+        t0 = const.tile([P, NH], F32, name="t0")
+        nc.vector.tensor_reduce(out=t0[:], in_=gn[:].rearrange("p j h -> p h j"), axis=AX.X, op=ALU.add)
+        nc.vector.tensor_scalar_mul(out=t0[:], in0=t0[:], scalar1=d3)
+        skf = const.tile([P, 2], F32, name="skf")
+        nc.vector.tensor_copy(out=skf[:], in_=skb[:])
+        nc.scalar.activation(out=sw[:], in_=skf[:], func=ACT.Sigmoid)
+
+        for hh in range(2):
+            lo = 64 * hh
+            nc.vector.tensor_copy(
+                out=csm[lo : lo + 64, :, 0:3], in_=pt[lo : lo + 64, 0:3, hh:NH:2].rearrange("p r i -> p i r")
+            )
+            nc.vector.tensor_copy(
+                out=csm[lo : lo + 64, :, 3:6], in_=rt[lo : lo + 64, 0:3, hh:NH:2].rearrange("p r i -> p i r")
+            )
+
+        fp = pre.tile([P, FROW], F32, name="fp", bufs=1)
+        nc.gpsimd.memset(fp[:], 0.0)
+        fv = fp[:, 0 : NH * 384].rearrange("p (h y) -> p h y", y=384)
+        big = [(0, t0[:])]
+        big += [(2**m, pt[:, m + 3, :]) for m in range(8)]
+        big += [(3 * 2**m, rt[:, m + 3, :]) for m in range(7)]
+        for sig, src in big:
+            for shift, scal in ((0, 1.0), (64, sw[:, 0:1]), (128, sw[:, 1:2])):
+                if sig + shift < NQ:
+                    pos = 128 + sig + shift
+                    nc.vector.scalar_tensor_tensor(
+                        out=fv[:, :, pos : pos + 1],
+                        in0=src.unsqueeze(2),
+                        scalar=scal,
+                        in1=fv[:, :, pos : pos + 1],
+                        op0=ALU.mult,
+                        op1=ALU.add,
+                    )
+        nc.scalar.dma_start(
+            out=oflat[TOEP_BASE : TOEP_BASE + P * FROW].rearrange("(p f) -> p f", f=FROW), in_=fp[:]
+        )
+        nc.scalar.dma_start(
+            out=wt[:],
+            in_=oflat[TOEP_BASE + 128 : TOEP_BASE + 128 + P * (FROW - 1)].rearrange(
+                "(p h y) -> p h y", h=NH, y=384
+            )[:, :, 0:NQ],
+        )
+
+        def mx_group(m, be):
+            acc = ps.tile([P, 512], F32, name="acc", tag="mx", bufs=2)
+            for g in range(2):
+                nc.tensor.matmul_mx(
+                    out=acc[:],
+                    lhsT=wc[:, g, P * m : P * m + P].bitcast(FP8X4),
+                    lhsT_scale=wsc[:, g, P * m : P * m + P],
+                    rhs=xc[:, g, 512 * be : 512 * be + 512].bitcast(FP8X4),
+                    rhs_scale=xsc[:, g, 512 * be : 512 * be + 512],
+                    start=(g == 0),
+                    stop=(g == 1),
+                )
+            return acc
+
+        st = {}
+
+        def keys(i):
+            ksq = main.tile([P, NTOK], F32, name="ksq", bufs=1)
+            st["ksq", i] = ksq
+            for be in range(4):
+                acc = mx_group(i, be)
+                nc.scalar.activation(
+                    out=ksq[:, 512 * be : 512 * be + 512], in_=acc[:], func=ACT.Square, bias=bT[:, i : i + 1]
+                )
+
+        def mag_a(i):
+            ksq = st["ksq", i]
+            msq = ps.tile([P, 32], F32, name="msq", tag="sm")
+            for j in range(16):
+                nc.tensor.matmul(
+                    out=msq[:, j:32:16], lhsT=ksq[:, P * j : P * j + P], rhs=ind[:], start=True, stop=True
+                )
+            nc.scalar.activation(out=magt[:, 0:32], in_=msq[:], func=ACT.Sqrt)
+
+        def mag_b(i):
+            mtp = ps.tile([P, P], F32, name="mtp", tag="sm")
+            nc.tensor.transpose(mtp[:], magt[:], ident[:])
+            mrow = main.tile([32, P], F32, name="mrow")
+            nc.scalar.copy(out=mrow[:], in_=mtp[0:32, :])
+            mb = MAG_BASE + 4096 * i
+            nc.sync.dma_start(out=oflat[mb : mb + 4096].rearrange("(r p) -> r p", p=P), in_=mrow[:])
+            magbc = main.tile([P, NTOK], F32, name="magbc", bufs=1)
+            st["magbc", i] = magbc
+            for hh in range(2):
+                nc.sync.dma_start(
+                    out=magbc[64 * hh : 64 * hh + 64, :],
+                    in_=oflat[mb + NTOK * hh : mb + NTOK * hh + NTOK].partition_broadcast(64),
+                )
+
+        def values(i, be):
+            st["v", i, be] = mx_group(8 + i, be)
+
+        def field(i, be):
+            nc.vector.scalar_tensor_tensor(
+                out=fts[i % 2][:, 2 * be : 2 * be + 2, HALO : HALO + NQ],
+                in0=st["v", i, be][:].rearrange("p (b q) -> p b q", b=2),
+                scalar=bT[:, 8 + i : 9 + i],
+                in1=st["magbc", i][:, 512 * be : 512 * be + 512].rearrange("p (b q) -> p b q", b=2),
+                op0=ALU.add,
+                op1=ALU.mult,
+            )
+
+        def first_tap(i, be):
+            ft = fts[i % 2]
+            if be == 0:
+                st["u", i] = main.tile([P, NB, NQ], F32, name="u")
+            u = st["u", i]
+            coef = csm[:, i, 0:1]
+            if be < 3:
+                nc.scalar.activation(
+                    out=u[:, 2 * be + 1 : 2 * be + 3, :], in_=ft[:, 2 * be : 2 * be + 2, HALO : HALO + NQ],
+                    func=ACT.Copy, scale=coef,
+                )
+            else:
+                nc.scalar.activation(out=u[:, 7:8, :], in_=ft[:, 6:7, HALO : HALO + NQ], func=ACT.Copy, scale=coef)
+                nc.scalar.activation(
+                    out=u[:, 0:1, :], in_=ft[:, 7:8, HALO - 1 : HALO - 1 + NQ], func=ACT.Copy, scale=coef
+                )
+
+        def chain(i):
+            ft = fts[i % 2]
+            u = st["u", i]
+            for r, ci in SMALL_TAPS[1:]:
+                rr, ex = r % NB, r // NB
+                coef = csm[:, i, ci : ci + 1]
+                parts = (
+                    (u[:, rr:NB, :], ft[:, 0 : NB - rr, HALO - ex : HALO - ex + NQ]),
+                    (u[:, 0:rr, :], ft[:, NB - rr : NB, HALO - 1 - ex : HALO - 1 - ex + NQ]),
+                )
+                for dst, src in parts:
+                    nc.vector.scalar_tensor_tensor(out=dst, in0=src, scalar=coef, in1=dst, op0=ALU.mult, op1=ALU.add)
+
+        def skips(i):
+            u = st["u", i]
+            up = main.tile([P, NB, NQ], F32, name="up", bufs=1)
+            st["up", i] = up
+            nc.scalar.copy(out=up[:, :, 0:64], in_=u[:, :, 0:64])
+            nc.vector.scalar_tensor_tensor(
+                out=up[:, :, 64:256], in0=u[:, :, 0:192], scalar=sw[:, 0:1], in1=u[:, :, 64:256],
+                op0=ALU.mult, op1=ALU.add,
+            )
+            nc.vector.scalar_tensor_tensor(
+                out=up[:, :, 128:256], in0=u[:, :, 0:128], scalar=sw[:, 1:2], in1=up[:, :, 128:256],
+                op0=ALU.mult, op1=ALU.add,
+            )
+
+        def field_to_tokens(i):
+            ft = fts[i % 2]
+            ftok = main.tile([P, 2, 2, NB, HD], F32, name="ftok", bufs=1)
+            st["ftok", i] = ftok
+            for t in range(2):
+                for hb in range(2):
+                    bank = ps.tile([P, 4, P], F32, name="bank", tag="tr", bufs=2)
+                    for b4 in range(4):
+                        c0 = HALO + P * t
+                        nc.tensor.transpose(bank[:, b4, :], ft[:, 4 * hb + b4, c0 : c0 + P], ident[:])
+                    nc.scalar.copy(
+                        out=ftok[:, t, :, 4 * hb : 4 * hb + 4, :],
+                        in_=bank[:].rearrange("p b (h c) -> p h b c", h=2),
+                    )
+
+        def toeplitz(i, t, hb, tag):
+            ftok = st["ftok", i]
+            ob = ps.tile([P, 4, P], F32, name="ob", tag=tag, bufs=(3 if tag == "ob" else 2))
+            st["ob", i, t, hb] = ob
+            first = True
+            for hh in range(2):
+                h = 2 * i + hh
+                for tin in range(t + 1):
+                    j0 = P * (t - tin)
+                    nc.tensor.matmul(
+                        out=ob[:, :, HD * hh : HD * hh + HD],
+                        lhsT=wt[:, h, j0 : j0 + P],
+                        rhs=ftok[:, tin, hh, 4 * hb : 4 * hb + 4, :],
+                        start=first,
+                        stop=False,
+                    )
+                    first = False
+
+        def finish(i, t, hb):
+            up = st["up", i]
+            ob = st["ob", i, t, hb]
+            if t == 0 and hb == 0:
+                st["ut", i] = main.tile([P, 2, 2, NB, HD], F32, name="ut", tag="ut", align_bytes=64)
+            ut = st["ut", i]
+            for b4 in range(4):
+                nc.tensor.matmul(
+                    out=ob[:, b4, :], lhsT=up[:, 4 * hb + b4, P * t : P * t + P], rhs=ident[:],
+                    is_transpose=True, start=False, stop=(b4 == 3),
+                )
+            nc.scalar.copy(
+                out=ut[:, t, :, 4 * hb : 4 * hb + 4, :], in_=ob[:].rearrange("p b (h c) -> p h b c", h=2)
+            )
+            if hb == 1:
+                nc.gpsimd.dma_start(
+                    out=oview[:, 2 * i : 2 * i + 2, t : t + 1, :].rearrange("p h o f -> p (h o) f"),
+                    in_=ut[:, t].rearrange("p h b c -> p h (b c)"),
+                )
+
+        with tc.manual_schedule():
+            keys(0)
+            mag_a(0)
+            mag_b(0)
+            keys(1)
+            values(0, 0)
+            values(0, 1)
+            for i in range(9):
+                last = i - 1 == 7
+                if i < 8:
+                    if i >= 1:
+                        toeplitz(i - 1, 0, 0, "ob")
+                    field(i, 0)
+                    first_tap(i, 0)
+                    values(i, 2)
+                    field(i, 1)
+                    first_tap(i, 1)
+                    values(i, 3)
+                    if i >= 1:
+                        toeplitz(i - 1, 0, 1, "ob")
+                    field(i, 2)
+                    first_tap(i, 2)
+                    field(i, 3)
+                    first_tap(i, 3)
+                if i >= 1:
+                    skips(i - 1)
+                if i < 8:
+                    chain(i)
+                if i + 1 < 8:
+                    mag_a(i + 1)
+                if i >= 1:
+                    finish(i - 1, 0, 0)
+                    finish(i - 1, 0, 1)
+                if i + 1 < 8:
+                    mag_b(i + 1)
+                if i == 0:
+                    quant_w(wst_c, 512, False)
+                    quant_w(wst_d, DM + 512, False)
+                if i >= 1:
+                    if not last:
+                        toeplitz(i - 1, 1, 0, "ob")
+                    finish(i - 1, 1, 0)
+                    if not last:
+                        toeplitz(i - 1, 1, 1, "ob")
+                    finish(i - 1, 1, 1)
+                if i < 8:
+                    field_to_tokens(i)
+                if i + 2 < 8:
+                    keys(i + 2)
+                if i + 1 < 8:
+                    values(i + 1, 0)
+                    values(i + 1, 1)
+                if i == 7:
+                    toeplitz(7, 0, 0, "ob")
+                    toeplitz(7, 0, 1, "ob")
+                    toeplitz(7, 1, 0, "ob")
+                    toeplitz(7, 1, 1, "tr")

@@ -38,13 +38,18 @@ def tile_causalwaveletfieldattentionh_pa_kernel(tc, x, Wkv, bkv, scale_gain, ski
 
     with ExitStack() as ctx:
         const = ctx.enter_context(tc.tile_pool(name="const", bufs=1))
-        wst_pool = ctx.enter_context(tc.tile_pool(name="wst", bufs=2))
-        pre = ctx.enter_context(tc.tile_pool(name="pre", bufs=2))
-        main = ctx.enter_context(tc.tile_pool(name="main", bufs=2))
+        sh = ctx.enter_context(tc.tile_pool(name="sh", bufs=2))
         ps = ctx.enter_context(tc.psum_pool(name="ps", bufs=1))
+        ctx.enter_context(tc.manual_schedule())
+
+        def slot(shape, dtype, name, tag):
+            return sh.tile(shape, dtype, name=name, tag=tag, bufs=(4 if tag in ("A", "B") else 2), align_bytes=64)
 
         ident = const.tile([P, P], F32, name="ident")
         make_identity(nc, ident[:])
+        fts = [const.tile([P, NB, HALO + NQ], F32, name="ft%d" % j) for j in range(2)]
+        for j in range(2):
+            nc.gpsimd.memset(fts[j][:, :, 0:HALO], 0.0)
         ind = const.tile([P, 2], F32, name="ind")
         nc.vector.memset(ind[:], 0.0)
         nc.vector.memset(ind[0:64, 0:1], 1.0)
@@ -53,9 +58,10 @@ def tile_causalwaveletfieldattentionh_pa_kernel(tc, x, Wkv, bkv, scale_gain, ski
         nc.vector.memset(magt[:], 0.0)
         bkf = const.tile([P, P], F32, name="bkf")
         nc.vector.memset(bkf[:], 0.0)
-        fts = [const.tile([P, NB, HALO + NQ], F32, name="ft%d" % j) for j in range(2)]
-        for j in range(2):
-            nc.gpsimd.memset(fts[j][:, :, 0:HALO], 0.0)
+        pt = const.tile([P, 11, NH], F32, name="pt")
+        nc.vector.memset(pt[:, 10:11, :], 0.0)
+        fp = const.tile([P, FROW], F32, name="fp")
+        nc.vector.memset(fp[:], 0.0)
 
         xc = const.tile([P, 2, NTOK], U32, name="xc", align_bytes=64)
         xsc = const.tile([P, 2, NTOK], U8, name="xsc", align_bytes=64)
@@ -74,7 +80,7 @@ def tile_causalwaveletfieldattentionh_pa_kernel(tc, x, Wkv, bkv, scale_gain, ski
         nc.sync.dma_start(out=bkb[:], in_=bkv.rearrange("(m c) -> m c", c=P))
 
         def load_w(c0):
-            wst = wst_pool.tile([P, 2, 4, 512], BF16, name="wst")
+            wst = slot([P, 2, 4, 512], BF16, "wst", "B")
             for g in range(2):
                 for u in range(2):
                     r0 = 512 * g + 256 * u
@@ -84,19 +90,13 @@ def tile_causalwaveletfieldattentionh_pa_kernel(tc, x, Wkv, bkv, scale_gain, ski
                     )
             return wst
 
-        def quant_w(wst, c0, on_vector):
-            if on_vector:
-                wg = wst_pool.tile([P, 2, 512, 4], BF16, name="wg", bufs=1, align_bytes=64)
-            else:
-                wg = main.tile([P, 2, 512, 4], BF16, name="wg2", tag="ut", align_bytes=64)
+        def quant_w(wst, c0):
+            wg = slot([P, 2, 512, 4], BF16, "wg", "D")
             for g in range(2):
-                if on_vector:
-                    nc.vector.tensor_copy(
-                        out=wg[:, g].rearrange("p (c i) t -> p c t i", i=4),
-                        in_=wst[:, g].rearrange("p t (c i) -> p c t i", i=4),
-                    )
-                else:
-                    nc.scalar.copy(out=wg[:, g], in_=wst[:, g].rearrange("p t c -> p c t"))
+                nc.vector.tensor_copy(
+                    out=wg[:, g].rearrange("p (c i) t -> p c t i", i=4),
+                    in_=wst[:, g].rearrange("p t (c i) -> p c t i", i=4),
+                )
             for g in range(2):
                 nc.vector.quantize_mx(
                     out=wc[:, g, c0 : c0 + 512].bitcast(FP8X4),
@@ -105,51 +105,14 @@ def tile_causalwaveletfieldattentionh_pa_kernel(tc, x, Wkv, bkv, scale_gain, ski
                 )
 
         def load_x(be):
-            xs = pre.tile([P, 2, 2, DM], BF16, name="xs")
+            xs = slot([P, 2, 2, DM], BF16, "xs", "A")
             nc.sync.dma_start(out=xs[:], in_=xview[:, :, 2 * be : 2 * be + 2, :])
             return xs
 
         wst_a = load_w(0)
-        xss = {0: load_x(0), 1: load_x(1)}
-
-        nc.vector.tensor_copy(out=bkf[0:16, :], in_=bkb[:])
-        bps = ps.tile([P, P], F32, name="bps", tag="sm")
-        nc.tensor.transpose(bps[:], bkf[:], ident[:])
-        nc.vector.tensor_copy(out=bT[:], in_=bps[:, 0:16])
-
-        quant_w(wst_a, 0, True)
-
-        for be in range(4):
-            xs = xss[be]
-            xg = pre.tile([P, 2, 512, 4], BF16, name="xg", align_bytes=64)
-            xg32 = xg[:].bitcast(F32)
-            for g in range(2):
-                for bb in range(2):
-                    xt = ps.tile([P, 2, 2, P], F32, name="xt", tag=("tr" if bb == 0 else "ob"), bufs=(2 if bb == 0 else 3))
-                    for t in range(2):
-                        xw = xs[:, t, bb, :].bitcast(F32)
-                        for u in range(2):
-                            w0 = 256 * g + 128 * u
-                            nc.tensor.transpose(xt[:, t, u, :], xw[:, w0 : w0 + 128], ident[:])
-                    dst = xg32[:, g, 256 * bb : 256 * bb + 256, :].rearrange("p (t k) u -> p t k u", t=2)
-                    src = xt[:].rearrange("p t u k -> p t k u")
-                    if bb == 0:
-                        nc.vector.tensor_copy(out=dst, in_=src)
-                    else:
-                        nc.scalar.copy(out=dst, in_=src)
-            if be + 2 < 4:
-                xss[be + 2] = load_x(be + 2)
-            if be == 1:
-                wst_b = load_w(DM)
-                wst_c = load_w(512)
-            for g in range(2):
-                nc.vector.quantize_mx(
-                    out=xc[:, g, 512 * be : 512 * be + 512].bitcast(FP8X4),
-                    scales=xsc[:, g, 512 * be : 512 * be + 512],
-                    in_=xg[:, g].rearrange("p c j -> p (c j)"),
-                )
-
-        quant_w(wst_b, DM, True)
+        xss = [load_x(be) for be in range(4)]
+        wst_b = load_w(DM)
+        wst_c = load_w(512)
         wst_d = load_w(DM + 512)
 
         sg = const.tile([P, 10, NH], F32, name="sg")
@@ -161,6 +124,14 @@ def tile_causalwaveletfieldattentionh_pa_kernel(tc, x, Wkv, bkv, scale_gain, ski
         )
         eg = const.tile([P, 10, NH], F32, name="eg")
         nc.scalar.activation(out=eg[:], in_=sg[:], func=ACT.Exp)
+        skf = const.tile([P, 2], F32, name="skf")
+        nc.vector.tensor_copy(out=skf[:], in_=skb[:])
+        nc.scalar.activation(out=sw[:], in_=skf[:], func=ACT.Sigmoid)
+        nc.vector.tensor_copy(out=bkf[0:16, :], in_=bkb[:])
+        bps = ps.tile([P, P], F32, name="bps", tag="sm")
+        nc.tensor.transpose(bps[:], bkf[:], ident[:])
+        nc.vector.tensor_copy(out=bT[:], in_=bps[:, 0:16])
+
         ssum = const.tile([P, NH], F32, name="ssum")
         nc.vector.tensor_reduce(out=ssum[:], in_=eg[:].rearrange("p j h -> p h j"), axis=AX.X, op=ALU.add)
         rsum = const.tile([P, NH], F32, name="rsum")
@@ -169,8 +140,6 @@ def tile_causalwaveletfieldattentionh_pa_kernel(tc, x, Wkv, bkv, scale_gain, ski
         nc.vector.tensor_tensor(
             out=gn[:], in0=eg[:], in1=rsum[:].unsqueeze(1).to_broadcast([P, 10, NH]), op=ALU.mult
         )
-        pt = const.tile([P, 11, NH], F32, name="pt")
-        nc.vector.memset(pt[:, 10:11, :], 0.0)
         nc.vector.tensor_scalar_mul(out=pt[:, 0:10, :], in0=gn[:], scalar1=d2)
         nc.vector.scalar_tensor_tensor(
             out=pt[:, 1:11, :], in0=gn[:], scalar=d1, in1=pt[:, 1:11, :], op0=ALU.mult, op1=ALU.add
@@ -180,10 +149,6 @@ def tile_causalwaveletfieldattentionh_pa_kernel(tc, x, Wkv, bkv, scale_gain, ski
         t0 = const.tile([P, NH], F32, name="t0")
         nc.vector.tensor_reduce(out=t0[:], in_=gn[:].rearrange("p j h -> p h j"), axis=AX.X, op=ALU.add)
         nc.vector.tensor_scalar_mul(out=t0[:], in0=t0[:], scalar1=d3)
-        skf = const.tile([P, 2], F32, name="skf")
-        nc.vector.tensor_copy(out=skf[:], in_=skb[:])
-        nc.scalar.activation(out=sw[:], in_=skf[:], func=ACT.Sigmoid)
-
         for hh in range(2):
             lo = 64 * hh
             nc.vector.tensor_copy(
@@ -193,33 +158,9 @@ def tile_causalwaveletfieldattentionh_pa_kernel(tc, x, Wkv, bkv, scale_gain, ski
                 out=csm[lo : lo + 64, :, 3:6], in_=rt[lo : lo + 64, 0:3, hh:NH:2].rearrange("p r i -> p i r")
             )
 
-        fp = pre.tile([P, FROW], F32, name="fp", bufs=1)
-        nc.gpsimd.memset(fp[:], 0.0)
-        fv = fp[:, 0 : NH * 384].rearrange("p (h y) -> p h y", y=384)
-        big = [(0, t0[:])]
-        big += [(2**m, pt[:, m + 3, :]) for m in range(8)]
-        big += [(3 * 2**m, rt[:, m + 3, :]) for m in range(7)]
-        for sig, src in big:
-            for shift, scal in ((0, 1.0), (64, sw[:, 0:1]), (128, sw[:, 1:2])):
-                if sig + shift < NQ:
-                    pos = 128 + sig + shift
-                    nc.vector.scalar_tensor_tensor(
-                        out=fv[:, :, pos : pos + 1],
-                        in0=src.unsqueeze(2),
-                        scalar=scal,
-                        in1=fv[:, :, pos : pos + 1],
-                        op0=ALU.mult,
-                        op1=ALU.add,
-                    )
-        nc.scalar.dma_start(
-            out=oflat[TOEP_BASE : TOEP_BASE + P * FROW].rearrange("(p f) -> p f", f=FROW), in_=fp[:]
-        )
-        nc.scalar.dma_start(
-            out=wt[:],
-            in_=oflat[TOEP_BASE + 128 : TOEP_BASE + 128 + P * (FROW - 1)].rearrange(
-                "(p h y) -> p h y", h=NH, y=384
-            )[:, :, 0:NQ],
-        )
+        quant_w(wst_a, 0)
+
+        st = {}
 
         def mx_group(m, be):
             acc = ps.tile([P, 512], F32, name="acc", tag="mx", bufs=2)
@@ -235,34 +176,34 @@ def tile_causalwaveletfieldattentionh_pa_kernel(tc, x, Wkv, bkv, scale_gain, ski
                 )
             return acc
 
-        st = {}
+        def keys(i, be):
+            if be == 0:
+                st["ksq", i] = slot([P, NTOK], F32, "ksq", "A")
+            acc = mx_group(i, be)
+            nc.scalar.activation(
+                out=st["ksq", i][:, 512 * be : 512 * be + 512], in_=acc[:], func=ACT.Square, bias=bT[:, i : i + 1]
+            )
 
-        def keys(i):
-            ksq = main.tile([P, NTOK], F32, name="ksq", bufs=1)
-            st["ksq", i] = ksq
-            for be in range(4):
-                acc = mx_group(i, be)
-                nc.scalar.activation(
-                    out=ksq[:, 512 * be : 512 * be + 512], in_=acc[:], func=ACT.Square, bias=bT[:, i : i + 1]
-                )
-
-        def mag_a(i):
+        def mag_a(i, be):
             ksq = st["ksq", i]
-            msq = ps.tile([P, 32], F32, name="msq", tag="sm")
-            for j in range(16):
+            if be == 0:
+                st["msq", i] = ps.tile([P, 32], F32, name="msq", tag="sm")
+            msq = st["msq", i]
+            for j in range(4 * be, 4 * be + 4):
                 nc.tensor.matmul(
                     out=msq[:, j:32:16], lhsT=ksq[:, P * j : P * j + P], rhs=ind[:], start=True, stop=True
                 )
-            nc.scalar.activation(out=magt[:, 0:32], in_=msq[:], func=ACT.Sqrt)
+            if be == 3:
+                nc.scalar.activation(out=magt[:, 0:32], in_=msq[:], func=ACT.Sqrt)
 
         def mag_b(i):
             mtp = ps.tile([P, P], F32, name="mtp", tag="sm")
             nc.tensor.transpose(mtp[:], magt[:], ident[:])
-            mrow = main.tile([32, P], F32, name="mrow")
+            mrow = sh.tile([32, P], F32, name="mrow")
             nc.scalar.copy(out=mrow[:], in_=mtp[0:32, :])
             mb = MAG_BASE + 4096 * i
-            nc.sync.dma_start(out=oflat[mb : mb + 4096].rearrange("(r p) -> r p", p=P), in_=mrow[:])
-            magbc = main.tile([P, NTOK], F32, name="magbc", bufs=1)
+            nc.scalar.dma_start(out=oflat[mb : mb + 4096].rearrange("(r p) -> r p", p=P), in_=mrow[:])
+            magbc = slot([P, NTOK], F32, "magbc", "A")
             st["magbc", i] = magbc
             for hh in range(2):
                 nc.sync.dma_start(
@@ -286,7 +227,7 @@ def tile_causalwaveletfieldattentionh_pa_kernel(tc, x, Wkv, bkv, scale_gain, ski
         def first_tap(i, be):
             ft = fts[i % 2]
             if be == 0:
-                st["u", i] = main.tile([P, NB, NQ], F32, name="u")
+                st["u", i] = slot([P, NB, NQ], F32, "u", "B")
             u = st["u", i]
             coef = csm[:, i, 0:1]
             if be < 3:
@@ -315,7 +256,7 @@ def tile_causalwaveletfieldattentionh_pa_kernel(tc, x, Wkv, bkv, scale_gain, ski
 
         def skips(i):
             u = st["u", i]
-            up = main.tile([P, NB, NQ], F32, name="up", bufs=1)
+            up = slot([P, NB, NQ], F32, "up", "B")
             st["up", i] = up
             nc.scalar.copy(out=up[:, :, 0:64], in_=u[:, :, 0:64])
             nc.vector.scalar_tensor_tensor(
@@ -327,20 +268,19 @@ def tile_causalwaveletfieldattentionh_pa_kernel(tc, x, Wkv, bkv, scale_gain, ski
                 op0=ALU.mult, op1=ALU.add,
             )
 
-        def field_to_tokens(i):
+        def field_to_tokens(i, t, hb):
             ft = fts[i % 2]
-            ftok = main.tile([P, 2, 2, NB, HD], F32, name="ftok", bufs=1)
-            st["ftok", i] = ftok
-            for t in range(2):
-                for hb in range(2):
-                    bank = ps.tile([P, 4, P], F32, name="bank", tag="tr", bufs=2)
-                    for b4 in range(4):
-                        c0 = HALO + P * t
-                        nc.tensor.transpose(bank[:, b4, :], ft[:, 4 * hb + b4, c0 : c0 + P], ident[:])
-                    nc.scalar.copy(
-                        out=ftok[:, t, :, 4 * hb : 4 * hb + 4, :],
-                        in_=bank[:].rearrange("p b (h c) -> p h b c", h=2),
-                    )
+            if t == 0 and hb == 0:
+                st["ftok", i] = slot([P, 2, 2, NB, HD], F32, "ftok", "C")
+            ftok = st["ftok", i]
+            bank = ps.tile([P, 4, P], F32, name="bank", tag="tr", bufs=2)
+            for b4 in range(4):
+                c0 = HALO + P * t
+                nc.tensor.transpose(bank[:, b4, :], ft[:, 4 * hb + b4, c0 : c0 + P], ident[:])
+            nc.scalar.copy(
+                out=ftok[:, t, :, 4 * hb : 4 * hb + 4, :],
+                in_=bank[:].rearrange("p b (h c) -> p h b c", h=2),
+            )
 
         def toeplitz(i, t, hb, tag):
             ftok = st["ftok", i]
@@ -364,7 +304,7 @@ def tile_causalwaveletfieldattentionh_pa_kernel(tc, x, Wkv, bkv, scale_gain, ski
             up = st["up", i]
             ob = st["ob", i, t, hb]
             if t == 0 and hb == 0:
-                st["ut", i] = main.tile([P, 2, 2, NB, HD], F32, name="ut", tag="ut", align_bytes=64)
+                st["ut", i] = slot([P, 2, 2, NB, HD], F32, "ut", "D")
             ut = st["ut", i]
             for b4 in range(4):
                 nc.tensor.matmul(
@@ -380,60 +320,122 @@ def tile_causalwaveletfieldattentionh_pa_kernel(tc, x, Wkv, bkv, scale_gain, ski
                     in_=ut[:, t].rearrange("p h b c -> p h (b c)"),
                 )
 
-        with tc.manual_schedule():
-            keys(0)
-            mag_a(0)
-            mag_b(0)
-            keys(1)
-            values(0, 0)
-            values(0, 1)
-            for i in range(9):
-                last = i - 1 == 7
-                if i < 8:
-                    if i >= 1:
-                        toeplitz(i - 1, 0, 0, "ob")
-                    field(i, 0)
-                    first_tap(i, 0)
-                    values(i, 2)
-                    field(i, 1)
-                    first_tap(i, 1)
-                    values(i, 3)
-                    if i >= 1:
-                        toeplitz(i - 1, 0, 1, "ob")
-                    field(i, 2)
-                    first_tap(i, 2)
-                    field(i, 3)
-                    first_tap(i, 3)
+        for be in range(4):
+            xs = xss[be]
+            xg = slot([P, 2, 512, 4], BF16, "xg", "C")
+            xg32 = xg[:].bitcast(F32)
+            for g in range(2):
+                for bb in range(2):
+                    xt = ps.tile([P, 2, 2, P], F32, name="xt", tag=("tr" if bb == 0 else "ob"), bufs=(2 if bb == 0 else 3))
+                    for t in range(2):
+                        xw = xs[:, t, bb, :].bitcast(F32)
+                        for u in range(2):
+                            w0 = 256 * g + 128 * u
+                            nc.tensor.transpose(xt[:, t, u, :], xw[:, w0 : w0 + 128], ident[:])
+                    dst = xg32[:, g, 256 * bb : 256 * bb + 256, :].rearrange("p (t k) u -> p t k u", t=2)
+                    src = xt[:].rearrange("p t u k -> p t k u")
+                    if bb == 0:
+                        nc.vector.tensor_copy(out=dst, in_=src)
+                    else:
+                        nc.scalar.copy(out=dst, in_=src)
+            if be >= 1:
+                keys(0, be - 1)
+            if be >= 2:
+                mag_a(0, be - 2)
+            for g in range(2):
+                nc.vector.quantize_mx(
+                    out=xc[:, g, 512 * be : 512 * be + 512].bitcast(FP8X4),
+                    scales=xsc[:, g, 512 * be : 512 * be + 512],
+                    in_=xg[:, g].rearrange("p c j -> p (c j)"),
+                )
+        keys(0, 3)
+        mag_a(0, 2)
+        mag_a(0, 3)
+        mag_b(0)
+
+        fv = fp[:, 0 : NH * 384].rearrange("p (h y) -> p h y", y=384)
+        big = [(0, t0[:])]
+        big += [(2**m, pt[:, m + 3, :]) for m in range(8)]
+        big += [(3 * 2**m, rt[:, m + 3, :]) for m in range(7)]
+        for sig, src in big:
+            for shift, scal in ((0, 1.0), (64, sw[:, 0:1]), (128, sw[:, 1:2])):
+                if sig + shift < NQ:
+                    pos = 128 + sig + shift
+                    nc.vector.scalar_tensor_tensor(
+                        out=fv[:, :, pos : pos + 1],
+                        in0=src.unsqueeze(2),
+                        scalar=scal,
+                        in1=fv[:, :, pos : pos + 1],
+                        op0=ALU.mult,
+                        op1=ALU.add,
+                    )
+        nc.gpsimd.dma_start(
+            out=oflat[TOEP_BASE : TOEP_BASE + P * FROW].rearrange("(p f) -> p f", f=FROW), in_=fp[:]
+        )
+        nc.gpsimd.dma_start(
+            out=wt[:],
+            in_=oflat[TOEP_BASE + 128 : TOEP_BASE + 128 + P * (FROW - 1)].rearrange(
+                "(p h y) -> p h y", h=NH, y=384
+            )[:, :, 0:NQ],
+        )
+        quant_w(wst_b, DM)
+        for be in range(4):
+            keys(1, be)
+        for be in range(4):
+            mag_a(1, be)
+        for be in range(4):
+            keys(2, be)
+        mag_b(1)
+        values(0, 0)
+        values(0, 1)
+        quant_w(wst_c, 512)
+        quant_w(wst_d, DM + 512)
+
+        for i in range(9):
+            if i < 8:
+                field(i, 0)
+                first_tap(i, 0)
+                values(i, 2)
+                field(i, 1)
+                first_tap(i, 1)
+                values(i, 3)
                 if i >= 1:
-                    skips(i - 1)
+                    toeplitz(i - 1, 0, 1, "ob")
+                field(i, 2)
+                first_tap(i, 2)
+                field(i, 3)
+                first_tap(i, 3)
+            if i + 2 < 8:
+                for be in range(4):
+                    mag_a(i + 2, be)
+            if 1 <= i < 8:
+                toeplitz(i - 1, 1, 0, "ob")
+            if i >= 1:
+                skips(i - 1)
+            if i < 8:
+                chain(i)
+            if i >= 1:
+                finish(i - 1, 0, 0)
+            if i + 2 < 8:
+                mag_b(i + 2)
+            if i >= 1:
+                finish(i - 1, 0, 1)
+                finish(i - 1, 1, 0)
                 if i < 8:
-                    chain(i)
-                if i + 1 < 8:
-                    mag_a(i + 1)
-                if i >= 1:
-                    finish(i - 1, 0, 0)
-                    finish(i - 1, 0, 1)
-                if i + 1 < 8:
-                    mag_b(i + 1)
-                if i == 0:
-                    quant_w(wst_c, 512, False)
-                    quant_w(wst_d, DM + 512, False)
-                if i >= 1:
-                    if not last:
-                        toeplitz(i - 1, 1, 0, "ob")
-                    finish(i - 1, 1, 0)
-                    if not last:
-                        toeplitz(i - 1, 1, 1, "ob")
-                    finish(i - 1, 1, 1)
-                if i < 8:
-                    field_to_tokens(i)
-                if i + 2 < 8:
-                    keys(i + 2)
-                if i + 1 < 8:
-                    values(i + 1, 0)
-                    values(i + 1, 1)
-                if i == 7:
-                    toeplitz(7, 0, 0, "ob")
-                    toeplitz(7, 0, 1, "ob")
-                    toeplitz(7, 1, 0, "ob")
-                    toeplitz(7, 1, 1, "tr")
+                    toeplitz(i - 1, 1, 1, "ob")
+                finish(i - 1, 1, 1)
+            if i < 8:
+                for half in range(2):
+                    field_to_tokens(i, half, 0)
+                    field_to_tokens(i, half, 1)
+                    if i + 3 < 8:
+                        keys(i + 3, 2 * half)
+                        keys(i + 3, 2 * half + 1)
+                toeplitz(i, 0, 0, "ob")
+            if i + 1 < 8:
+                values(i + 1, 0)
+                values(i + 1, 1)
+            if i == 7:
+                toeplitz(7, 0, 1, "ob")
+                toeplitz(7, 1, 0, "ob")
+                toeplitz(7, 1, 1, "tr")

@@ -27,6 +27,7 @@ FROW = NH * 384 + 1
 TOEP_BASE = 9 * NTOK * HD
 MAG_BASE = 15 * NTOK * HD + NTOK * HD // 2
 SMALL_TAPS = ((1, 0), (2, 1), (3, 3), (4, 2), (6, 4), (12, 5))
+PSB = {"v": 2, "k": 1, "tr": 1, "ob": 2, "sm": 1, "mt": 1}
 
 
 def tile_causalwaveletfieldattentionh_pa_kernel(tc, x, Wkv, bkv, scale_gain, skip_w, out):
@@ -43,7 +44,7 @@ def tile_causalwaveletfieldattentionh_pa_kernel(tc, x, Wkv, bkv, scale_gain, ski
         ctx.enter_context(tc.manual_schedule())
 
         def slot(shape, dtype, name, tag):
-            return sh.tile(shape, dtype, name=name, tag=tag, bufs=(4 if tag in ("A", "B") else 2), align_bytes=64)
+            return sh.tile(shape, dtype, name=name, tag=tag, bufs=(4 if tag == "B" else 2), align_bytes=64)
 
         ident = const.tile([P, P], F32, name="ident")
         make_identity(nc, ident[:])
@@ -105,7 +106,7 @@ def tile_causalwaveletfieldattentionh_pa_kernel(tc, x, Wkv, bkv, scale_gain, ski
                 )
 
         def load_x(be):
-            xs = slot([P, 2, 2, DM], BF16, "xs", "A")
+            xs = slot([P, 2, 2, DM], BF16, "xs", "AE"[be % 2])
             nc.sync.dma_start(out=xs[:], in_=xview[:, :, 2 * be : 2 * be + 2, :])
             return xs
 
@@ -162,8 +163,8 @@ def tile_causalwaveletfieldattentionh_pa_kernel(tc, x, Wkv, bkv, scale_gain, ski
 
         st = {}
 
-        def mx_group(m, be):
-            acc = ps.tile([P, 512], F32, name="acc", tag="mx", bufs=2)
+        def mx_group(m, be, tag):
+            acc = ps.tile([P, 512], F32, name="acc", tag=tag, bufs=PSB[tag])
             for g in range(2):
                 nc.tensor.matmul_mx(
                     out=acc[:],
@@ -176,10 +177,10 @@ def tile_causalwaveletfieldattentionh_pa_kernel(tc, x, Wkv, bkv, scale_gain, ski
                 )
             return acc
 
-        def keys(i, be):
+        def keys(i, be, tag="k"):
             if be == 0:
                 st["ksq", i] = slot([P, NTOK], F32, "ksq", "A")
-            acc = mx_group(i, be)
+            acc = mx_group(i, be, tag)
             nc.scalar.activation(
                 out=st["ksq", i][:, 512 * be : 512 * be + 512], in_=acc[:], func=ACT.Square, bias=bT[:, i : i + 1]
             )
@@ -197,13 +198,16 @@ def tile_causalwaveletfieldattentionh_pa_kernel(tc, x, Wkv, bkv, scale_gain, ski
                 nc.scalar.activation(out=magt[:, 0:32], in_=msq[:], func=ACT.Sqrt)
 
         def mag_b(i):
-            mtp = ps.tile([P, P], F32, name="mtp", tag="sm")
+            mtp = ps.tile([P, P], F32, name="mtp", tag="mt")
             nc.tensor.transpose(mtp[:], magt[:], ident[:])
             mrow = sh.tile([32, P], F32, name="mrow")
             nc.scalar.copy(out=mrow[:], in_=mtp[0:32, :])
             mb = MAG_BASE + 4096 * i
             nc.scalar.dma_start(out=oflat[mb : mb + 4096].rearrange("(r p) -> r p", p=P), in_=mrow[:])
-            magbc = slot([P, NTOK], F32, "magbc", "A")
+
+        def mag_c(i):
+            mb = MAG_BASE + 4096 * i
+            magbc = slot([P, NTOK], F32, "magbc", "E")
             st["magbc", i] = magbc
             for hh in range(2):
                 nc.sync.dma_start(
@@ -212,7 +216,7 @@ def tile_causalwaveletfieldattentionh_pa_kernel(tc, x, Wkv, bkv, scale_gain, ski
                 )
 
         def values(i, be):
-            st["v", i, be] = mx_group(8 + i, be)
+            st["v", i, be] = mx_group(8 + i, be, "v")
 
         def field(i, be):
             nc.vector.scalar_tensor_tensor(
@@ -241,18 +245,18 @@ def tile_causalwaveletfieldattentionh_pa_kernel(tc, x, Wkv, bkv, scale_gain, ski
                     out=u[:, 0:1, :], in_=ft[:, 7:8, HALO - 1 : HALO - 1 + NQ], func=ACT.Copy, scale=coef
                 )
 
-        def chain(i):
+        def chain(i, tap, part):
             ft = fts[i % 2]
             u = st["u", i]
-            for r, ci in SMALL_TAPS[1:]:
-                rr, ex = r % NB, r // NB
-                coef = csm[:, i, ci : ci + 1]
-                parts = (
-                    (u[:, rr:NB, :], ft[:, 0 : NB - rr, HALO - ex : HALO - ex + NQ]),
-                    (u[:, 0:rr, :], ft[:, NB - rr : NB, HALO - 1 - ex : HALO - 1 - ex + NQ]),
-                )
-                for dst, src in parts:
-                    nc.vector.scalar_tensor_tensor(out=dst, in0=src, scalar=coef, in1=dst, op0=ALU.mult, op1=ALU.add)
+            r, ci = SMALL_TAPS[tap]
+            rr, ex = r % NB, r // NB
+            if part == 0:
+                dst, src = u[:, rr:NB, :], ft[:, 0 : NB - rr, HALO - ex : HALO - ex + NQ]
+            else:
+                dst, src = u[:, 0:rr, :], ft[:, NB - rr : NB, HALO - 1 - ex : HALO - 1 - ex + NQ]
+            nc.vector.scalar_tensor_tensor(
+                out=dst, in0=src, scalar=csm[:, i, ci : ci + 1], in1=dst, op0=ALU.mult, op1=ALU.add
+            )
 
         def skips(i):
             u = st["u", i]
@@ -273,7 +277,7 @@ def tile_causalwaveletfieldattentionh_pa_kernel(tc, x, Wkv, bkv, scale_gain, ski
             if t == 0 and hb == 0:
                 st["ftok", i] = slot([P, 2, 2, NB, HD], F32, "ftok", "C")
             ftok = st["ftok", i]
-            bank = ps.tile([P, 4, P], F32, name="bank", tag="tr", bufs=2)
+            bank = ps.tile([P, 4, P], F32, name="bank", tag="tr", bufs=PSB["tr"])
             for b4 in range(4):
                 c0 = HALO + P * t
                 nc.tensor.transpose(bank[:, b4, :], ft[:, 4 * hb + b4, c0 : c0 + P], ident[:])
@@ -284,7 +288,7 @@ def tile_causalwaveletfieldattentionh_pa_kernel(tc, x, Wkv, bkv, scale_gain, ski
 
         def toeplitz(i, t, hb, tag):
             ftok = st["ftok", i]
-            ob = ps.tile([P, 4, P], F32, name="ob", tag=tag, bufs=(3 if tag == "ob" else 2))
+            ob = ps.tile([P, 4, P], F32, name="ob", tag=tag, bufs=PSB[tag])
             st["ob", i, t, hb] = ob
             first = True
             for hh in range(2):
@@ -326,7 +330,8 @@ def tile_causalwaveletfieldattentionh_pa_kernel(tc, x, Wkv, bkv, scale_gain, ski
             xg32 = xg[:].bitcast(F32)
             for g in range(2):
                 for bb in range(2):
-                    xt = ps.tile([P, 2, 2, P], F32, name="xt", tag=("tr" if bb == 0 else "ob"), bufs=(2 if bb == 0 else 3))
+                    xtag = ("tr", "ob", "ob", "mt")[2 * g + bb]
+                    xt = ps.tile([P, 2, 2, P], F32, name="xt", tag=xtag, bufs=PSB[xtag])
                     for t in range(2):
                         xw = xs[:, t, bb, :].bitcast(F32)
                         for u in range(2):
@@ -334,12 +339,12 @@ def tile_causalwaveletfieldattentionh_pa_kernel(tc, x, Wkv, bkv, scale_gain, ski
                             nc.tensor.transpose(xt[:, t, u, :], xw[:, w0 : w0 + 128], ident[:])
                     dst = xg32[:, g, 256 * bb : 256 * bb + 256, :].rearrange("p (t k) u -> p t k u", t=2)
                     src = xt[:].rearrange("p t u k -> p t k u")
-                    if bb == 0:
+                    if g == 0 and bb == 0:
                         nc.vector.tensor_copy(out=dst, in_=src)
                     else:
                         nc.scalar.copy(out=dst, in_=src)
             if be >= 1:
-                keys(0, be - 1)
+                keys(0, be - 1, "kv"[be % 2])
             if be >= 2:
                 mag_a(0, be - 2)
             for g in range(2):
@@ -348,11 +353,58 @@ def tile_causalwaveletfieldattentionh_pa_kernel(tc, x, Wkv, bkv, scale_gain, ski
                     scales=xsc[:, g, 512 * be : 512 * be + 512],
                     in_=xg[:, g].rearrange("p c j -> p (c j)"),
                 )
-        keys(0, 3)
+        keys(0, 3, "k")
         mag_a(0, 2)
         mag_a(0, 3)
         mag_b(0)
+        mag_c(0)
 
+        CHAIN_ROUNDS = (((1, 0), (1, 1)), ((2, 0), (2, 1), (3, 0)), ((3, 1), (4, 0), (4, 1)), ((5, 0), (5, 1)))
+        LAST_TAGS = ("v", "v", "k", "tr")
+
+        def period(i):
+            for r in range(4):
+                t, hb = r // 2, r % 2
+                if 0 <= i + 1 < 8:
+                    values(i + 1, r)
+                if 4 <= i + 4 < 8:
+                    keys(i + 4, r)
+                if 0 <= i < 8:
+                    field_to_tokens(i, t, hb)
+                if 0 <= i - 1 < 7:
+                    toeplitz(i - 1, t, hb, "ob")
+                if 0 <= i - 1 < 8:
+                    finish(i - 1, t, hb)
+                if r == 3 and 3 <= i + 3 < 8:
+                    mag_b(i + 3)
+                if 3 <= i + 3 < 8 and r < 3:
+                    mag_a(i + 3, r)
+                    if r == 2:
+                        mag_a(i + 3, 3)
+                if 0 <= i < 8:
+                    for tap, part in CHAIN_ROUNDS[r]:
+                        chain(i, tap, part)
+                if 0 <= i + 1 < 8:
+                    field(i + 1, r)
+                    first_tap(i + 1, r)
+                if r == 3 and 2 <= i + 3 < 8:
+                    mag_c(i + 3)
+                if r == 3 and 0 <= i < 8:
+                    skips(i)
+            if i == 7:
+                for r in range(4):
+                    toeplitz(7, r // 2, r % 2, LAST_TAGS[r])
+
+        for j in (1, 2, 3):
+            for be in range(4):
+                keys(j, be, ("k", "ob", "ob", "tr")[be])
+            if j < 3:
+                for be in range(4):
+                    mag_a(j, be)
+            if j < 3:
+                mag_b(j)
+            if j == 1:
+                mag_c(1)
         fv = fp[:, 0 : NH * 384].rearrange("p (h y) -> p h y", y=384)
         big = [(0, t0[:])]
         big += [(2**m, pt[:, m + 3, :]) for m in range(8)]
@@ -379,63 +431,7 @@ def tile_causalwaveletfieldattentionh_pa_kernel(tc, x, Wkv, bkv, scale_gain, ski
             )[:, :, 0:NQ],
         )
         quant_w(wst_b, DM)
-        for be in range(4):
-            keys(1, be)
-        for be in range(4):
-            mag_a(1, be)
-        for be in range(4):
-            keys(2, be)
-        mag_b(1)
-        values(0, 0)
-        values(0, 1)
         quant_w(wst_c, 512)
         quant_w(wst_d, DM + 512)
-
-        for i in range(9):
-            if i < 8:
-                field(i, 0)
-                first_tap(i, 0)
-                values(i, 2)
-                field(i, 1)
-                first_tap(i, 1)
-                values(i, 3)
-                if i >= 1:
-                    toeplitz(i - 1, 0, 1, "ob")
-                field(i, 2)
-                first_tap(i, 2)
-                field(i, 3)
-                first_tap(i, 3)
-            if i + 2 < 8:
-                for be in range(4):
-                    mag_a(i + 2, be)
-            if 1 <= i < 8:
-                toeplitz(i - 1, 1, 0, "ob")
-            if i >= 1:
-                skips(i - 1)
-            if i < 8:
-                chain(i)
-            if i >= 1:
-                finish(i - 1, 0, 0)
-            if i + 2 < 8:
-                mag_b(i + 2)
-            if i >= 1:
-                finish(i - 1, 0, 1)
-                finish(i - 1, 1, 0)
-                if i < 8:
-                    toeplitz(i - 1, 1, 1, "ob")
-                finish(i - 1, 1, 1)
-            if i < 8:
-                for half in range(2):
-                    field_to_tokens(i, half, 0)
-                    field_to_tokens(i, half, 1)
-                    if i + 3 < 8:
-                        keys(i + 3, 2 * half)
-                        keys(i + 3, 2 * half + 1)
-                toeplitz(i, 0, 0, "ob")
-            if i + 1 < 8:
-                values(i + 1, 0)
-                values(i + 1, 1)
-            if i == 7:
-                toeplitz(7, 0, 1, "ob")
-                toeplitz(7, 1, 0, "ob")
-                toeplitz(7, 1, 1, "tr")
+        for i in range(-1, 9):
+            period(i)

@@ -40,14 +40,17 @@ def tile_causalwaveletfieldattentionh_pa_kernel(tc, x, Wkv, bkv, scale_gain, ski
     with ExitStack() as ctx:
         const = ctx.enter_context(tc.tile_pool(name="const", bufs=1))
         sh = ctx.enter_context(tc.tile_pool(name="sh", bufs=2))
+        ov = ctx.enter_context(tc.tile_pool(name="ov", bufs=1))
         ps = ctx.enter_context(tc.psum_pool(name="ps", bufs=1))
         ctx.enter_context(tc.manual_schedule())
 
         def slot(shape, dtype, name, tag):
-            return sh.tile(shape, dtype, name=name, tag=tag, bufs=(4 if tag == "B" else 2), align_bytes=64)
+            return sh.tile(shape, dtype, name=name, tag=tag, bufs=2, align_bytes=64)
 
         ident = const.tile([P, P], F32, name="ident")
         make_identity(nc, ident[:])
+        fp = ov.tile([P, FROW], F32, name="fp", offset=0)
+        nc.gpsimd.memset(fp[:], 0.0)
         fts = [const.tile([P, NB, HALO + NQ], F32, name="ft%d" % j) for j in range(2)]
         for j in range(2):
             nc.gpsimd.memset(fts[j][:, :, 0:HALO], 0.0)
@@ -61,13 +64,14 @@ def tile_causalwaveletfieldattentionh_pa_kernel(tc, x, Wkv, bkv, scale_gain, ski
         nc.vector.memset(bkf[:], 0.0)
         pt = const.tile([P, 11, NH], F32, name="pt")
         nc.vector.memset(pt[:, 10:11, :], 0.0)
-        fp = const.tile([P, FROW], F32, name="fp")
-        nc.vector.memset(fp[:], 0.0)
+        warm = const.tile([P, 1], F32, name="warm")
+        nc.vector.memset(warm[:], 1.0)
 
         xc = const.tile([P, 2, NTOK], U32, name="xc", align_bytes=64)
         xsc = const.tile([P, 2, NTOK], U8, name="xsc", align_bytes=64)
-        wc = const.tile([P, 2, 2 * DM], U32, name="wc", align_bytes=64)
-        wsc = const.tile([P, 2, 2 * DM], U8, name="wsc", align_bytes=64)
+        wc = const.tile([P, 16, 2, P], U32, name="wc", align_bytes=64)
+        wsc = const.tile([P, 16, 2, P], U8, name="wsc", align_bytes=64)
+        wraw = const.tile([P, 2, 4, 2 * DM], BF16, name="wraw")
         wt = const.tile([P, NH, NQ], F32, name="wt")
         bT = const.tile([P, 16], F32, name="bT")
         csm = const.tile([P, 8, 6], F32, name="csm")
@@ -80,41 +84,44 @@ def tile_causalwaveletfieldattentionh_pa_kernel(tc, x, Wkv, bkv, scale_gain, ski
         bkb = const.tile([16, P], BF16, name="bkb")
         nc.sync.dma_start(out=bkb[:], in_=bkv.rearrange("(m c) -> m c", c=P))
 
-        def load_w(c0):
-            wst = slot([P, 2, 4, 512], BF16, "wst", "B")
+        def load_w(c0, c1):
             for g in range(2):
                 for u in range(2):
                     r0 = 512 * g + 256 * u
                     nc.sync.dma_start(
-                        out=wst[:, g, 2 * u : 2 * u + 2, :],
-                        in_=Wkv[r0 : r0 + 256, c0 : c0 + 512].rearrange("(p e) c -> p e c", e=2),
+                        out=wraw[:, g, 2 * u : 2 * u + 2, c0:c1],
+                        in_=Wkv[r0 : r0 + 256, c0:c1].rearrange("(p e) c -> p e c", e=2),
                     )
-            return wst
 
-        def quant_w(wst, c0):
-            wg = slot([P, 2, 512, 4], BF16, "wg", "D")
-            for g in range(2):
-                nc.vector.tensor_copy(
-                    out=wg[:, g].rearrange("p (c i) t -> p c t i", i=4),
-                    in_=wst[:, g].rearrange("p t (c i) -> p c t i", i=4),
-                )
-            for g in range(2):
-                nc.vector.quantize_mx(
-                    out=wc[:, g, c0 : c0 + 512].bitcast(FP8X4),
-                    scales=wsc[:, g, c0 : c0 + 512],
-                    in_=wg[:, g].rearrange("p c t -> p (c t)"),
-                )
+        def regroup_w(m, on_vector):
+            wg = sh.tile([P, 2, P, 4], BF16, name="wg", bufs=3, align_bytes=64)
+            st["wg", m] = wg
+            src = wraw[:, :, :, P * m : P * m + P].rearrange("p g t c -> p g c t")
+            if on_vector:
+                nc.vector.tensor_copy(out=wg[:], in_=src)
+            else:
+                nc.scalar.copy(out=wg[:], in_=src)
+
+        def quant_w(m):
+            nc.vector.quantize_mx(
+                out=wc[:, m].rearrange("p g c -> p (g c)").bitcast(FP8X4),
+                scales=wsc[:, m].rearrange("p g c -> p (g c)"),
+                in_=st["wg", m][:].rearrange("p g c t -> p (g c t)"),
+            )
 
         def load_x(be):
             xs = slot([P, 2, 2, DM], BF16, "xs", "AE"[be % 2])
             nc.sync.dma_start(out=xs[:], in_=xview[:, :, 2 * be : 2 * be + 2, :])
             return xs
 
-        wst_a = load_w(0)
+        st = {}
+        load_w(0, P)
         xss = [load_x(be) for be in range(4)]
-        wst_b = load_w(DM)
-        wst_c = load_w(512)
-        wst_d = load_w(DM + 512)
+        load_w(DM, DM + P)
+        load_w(P, 512)
+        load_w(DM + P, DM + 512)
+        load_w(512, DM)
+        load_w(DM + 512, 2 * DM)
 
         sg = const.tile([P, 10, NH], F32, name="sg")
         nc.vector.tensor_copy(out=sg[:].rearrange("p j h -> p (j h)"), in_=sgb[:])
@@ -127,11 +134,14 @@ def tile_causalwaveletfieldattentionh_pa_kernel(tc, x, Wkv, bkv, scale_gain, ski
         nc.scalar.activation(out=eg[:], in_=sg[:], func=ACT.Exp)
         skf = const.tile([P, 2], F32, name="skf")
         nc.vector.tensor_copy(out=skf[:], in_=skb[:])
-        nc.scalar.activation(out=sw[:], in_=skf[:], func=ACT.Sigmoid)
+        nc.scalar.activation(out=skf[:], in_=skf[:], func=ACT.Exp, scale=-1.0)
+        nc.scalar.activation(out=warm[:], in_=warm[:], func=ACT.Sqrt)
         nc.vector.tensor_copy(out=bkf[0:16, :], in_=bkb[:])
         bps = ps.tile([P, P], F32, name="bps", tag="sm")
         nc.tensor.transpose(bps[:], bkf[:], ident[:])
         nc.vector.tensor_copy(out=bT[:], in_=bps[:, 0:16])
+        regroup_w(0, True)
+        quant_w(0)
 
         ssum = const.tile([P, NH], F32, name="ssum")
         nc.vector.tensor_reduce(out=ssum[:], in_=eg[:].rearrange("p j h -> p h j"), axis=AX.X, op=ALU.add)
@@ -150,6 +160,8 @@ def tile_causalwaveletfieldattentionh_pa_kernel(tc, x, Wkv, bkv, scale_gain, ski
         t0 = const.tile([P, NH], F32, name="t0")
         nc.vector.tensor_reduce(out=t0[:], in_=gn[:].rearrange("p j h -> p h j"), axis=AX.X, op=ALU.add)
         nc.vector.tensor_scalar_mul(out=t0[:], in0=t0[:], scalar1=d3)
+        nc.vector.tensor_scalar_add(out=skf[:], in0=skf[:], scalar1=1.0)
+        nc.vector.reciprocal(out=sw[:], in_=skf[:])
         for hh in range(2):
             lo = 64 * hh
             nc.vector.tensor_copy(
@@ -159,17 +171,46 @@ def tile_causalwaveletfieldattentionh_pa_kernel(tc, x, Wkv, bkv, scale_gain, ski
                 out=csm[lo : lo + 64, :, 3:6], in_=rt[lo : lo + 64, 0:3, hh:NH:2].rearrange("p r i -> p i r")
             )
 
-        quant_w(wst_a, 0)
+        big = [(0, t0[:])]
+        big += [(2**m, pt[:, m + 3, :]) for m in range(8)]
+        big += [(3 * 2**m, rt[:, m + 3, :]) for m in range(7)]
+        toep_ops = []
+        for sig, src in big:
+            for shift, scal in ((0, 1.0), (64, sw[:, 0:1]), (128, sw[:, 1:2])):
+                if sig + shift < NQ:
+                    toep_ops.append((128 + sig + shift, src, scal))
 
-        st = {}
+        fv = fp[:, 0 : NH * 384].rearrange("p (h y) -> p h y", y=384)
+
+        def toep_fill(lo, hi):
+            for pos, src, scal in toep_ops[lo:hi]:
+                nc.vector.scalar_tensor_tensor(
+                    out=fv[:, :, pos : pos + 1],
+                    in0=src.unsqueeze(2),
+                    scalar=scal,
+                    in1=fv[:, :, pos : pos + 1],
+                    op0=ALU.mult,
+                    op1=ALU.add,
+                )
+
+        def toep_dma():
+            nc.gpsimd.dma_start(
+                out=oflat[TOEP_BASE : TOEP_BASE + P * FROW].rearrange("(p f) -> p f", f=FROW), in_=fp[:]
+            )
+            nc.gpsimd.dma_start(
+                out=wt[:],
+                in_=oflat[TOEP_BASE + 128 : TOEP_BASE + 128 + P * (FROW - 1)].rearrange(
+                    "(p h y) -> p h y", h=NH, y=384
+                )[:, :, 0:NQ],
+            )
 
         def mx_group(m, be, tag):
             acc = ps.tile([P, 512], F32, name="acc", tag=tag, bufs=PSB[tag])
             for g in range(2):
                 nc.tensor.matmul_mx(
                     out=acc[:],
-                    lhsT=wc[:, g, P * m : P * m + P].bitcast(FP8X4),
-                    lhsT_scale=wsc[:, g, P * m : P * m + P],
+                    lhsT=wc[:, m, g, :].bitcast(FP8X4),
+                    lhsT_scale=wsc[:, m, g, :],
                     rhs=xc[:, g, 512 * be : 512 * be + 512].bitcast(FP8X4),
                     rhs_scale=xsc[:, g, 512 * be : 512 * be + 512],
                     start=(g == 0),
@@ -194,8 +235,29 @@ def tile_causalwaveletfieldattentionh_pa_kernel(tc, x, Wkv, bkv, scale_gain, ski
                 nc.tensor.matmul(
                     out=msq[:, j:32:16], lhsT=ksq[:, P * j : P * j + P], rhs=ind[:], start=True, stop=True
                 )
-            if be == 3:
+            if be == 3 and i >= 2:
                 nc.scalar.activation(out=magt[:, 0:32], in_=msq[:], func=ACT.Sqrt)
+
+        def mag_r(i, be):
+            rep = sh.tile([P, 4, P], F32, name="rep", bufs=2)
+            st["rep", i, be] = rep
+            src = st["msq", i][:].rearrange("p (h j) -> p j h", h=2)[:, 4 * be : 4 * be + 4, :]
+            nc.scalar.activation(
+                out=rep[:].rearrange("p j (h c) -> p j h c", h=2),
+                in_=src.unsqueeze(3).to_broadcast([P, 4, 2, HD]),
+                func=ACT.Sqrt,
+            )
+
+        def mag_t(i, be, tag):
+            if be == 0:
+                st["magbc", i] = slot([P, NTOK], F32, "magbc", "E")
+            rep = st["rep", i, be]
+            bank = ps.tile([P, 4, P], F32, name="mbank", tag=tag, bufs=PSB[tag])
+            for j4 in range(4):
+                nc.tensor.transpose(bank[:, j4, :], rep[:, j4, :], ident[:])
+            nc.scalar.copy(
+                out=st["magbc", i][:, 512 * be : 512 * be + 512], in_=bank[:].rearrange("p j t -> p (j t)")
+            )
 
         def mag_b(i):
             mtp = ps.tile([P, P], F32, name="mtp", tag="mt")
@@ -260,7 +322,7 @@ def tile_causalwaveletfieldattentionh_pa_kernel(tc, x, Wkv, bkv, scale_gain, ski
 
         def skips(i):
             u = st["u", i]
-            up = slot([P, NB, NQ], F32, "up", "B")
+            up = ov.tile([P, NB, NQ], F32, name="up", tag="up", bufs=2, offset=16384)
             st["up", i] = up
             nc.scalar.copy(out=up[:, :, 0:64], in_=u[:, :, 0:64])
             nc.vector.scalar_tensor_tensor(
@@ -308,7 +370,7 @@ def tile_causalwaveletfieldattentionh_pa_kernel(tc, x, Wkv, bkv, scale_gain, ski
             up = st["up", i]
             ob = st["ob", i, t, hb]
             if t == 0 and hb == 0:
-                st["ut", i] = slot([P, 2, 2, NB, HD], F32, "ut", "D")
+                st["ut", i] = ov.tile([P, 2, 2, NB, HD], F32, name="ut", tag="ut", bufs=2, offset=0)
             ut = st["ut", i]
             for b4 in range(4):
                 nc.tensor.matmul(
@@ -324,7 +386,7 @@ def tile_causalwaveletfieldattentionh_pa_kernel(tc, x, Wkv, bkv, scale_gain, ski
                     in_=ut[:, t].rearrange("p h b c -> p h (b c)"),
                 )
 
-        for be in range(4):
+        def x_chunk(be):
             xs = xss[be]
             xg = slot([P, 2, 512, 4], BF16, "xg", "C")
             xg32 = xg[:].bitcast(F32)
@@ -343,21 +405,72 @@ def tile_causalwaveletfieldattentionh_pa_kernel(tc, x, Wkv, bkv, scale_gain, ski
                         nc.vector.tensor_copy(out=dst, in_=src)
                     else:
                         nc.scalar.copy(out=dst, in_=src)
-            if be >= 1:
-                keys(0, be - 1, "kv"[be % 2])
-            if be >= 2:
-                mag_a(0, be - 2)
+            return xg
+
+        def x_quant(be, xg):
             for g in range(2):
                 nc.vector.quantize_mx(
                     out=xc[:, g, 512 * be : 512 * be + 512].bitcast(FP8X4),
                     scales=xsc[:, g, 512 * be : 512 * be + 512],
                     in_=xg[:, g].rearrange("p c j -> p (c j)"),
                 )
-        keys(0, 3, "k")
-        mag_a(0, 2)
-        mag_a(0, 3)
-        mag_b(0)
-        mag_c(0)
+
+        for it in range(7):
+            if it < 4:
+                xg = x_chunk(it)
+            if 1 <= it <= 4:
+                keys(0, it - 1, "k")
+            if 2 <= it <= 5:
+                mag_a(0, it - 2)
+                mag_r(0, it - 2)
+            if 3 <= it <= 6:
+                mag_t(0, it - 3, "v")
+            if it < 4:
+                x_quant(it, xg)
+                toep_fill(12 * it, 12 * it + 12)
+            if it == 3:
+                toep_dma()
+            if it == 4:
+                regroup_w(8, True)
+                quant_w(8)
+                regroup_w(1, True)
+                quant_w(1)
+            if it >= 4:
+                keys(1, it - 4, ("ob", "ob", "tr")[it - 4])
+        values(0, 0)
+        keys(1, 3, "mt")
+        values(0, 1)
+        for m in (9, 2, 3, 4, 10):
+            regroup_w(m, True)
+            quant_w(m)
+        field(0, 0)
+        first_tap(0, 0)
+        values(0, 2)
+        field(0, 1)
+        first_tap(0, 1)
+        values(0, 3)
+        for be in range(4):
+            mag_a(1, be)
+        field(0, 2)
+        first_tap(0, 2)
+        values(1, 0)
+        field(0, 3)
+        first_tap(0, 3)
+        values(1, 1)
+        mag_r(1, 0)
+        mag_r(1, 1)
+        mag_t(1, 0, "ob")
+        keys(2, 0, "k")
+        mag_r(1, 2)
+        mag_t(1, 1, "ob")
+        keys(2, 1, "tr")
+        mag_r(1, 3)
+        mag_t(1, 2, "ob")
+        keys(2, 2, "mt")
+        keys(2, 3, "k")
+        mag_t(1, 3, "ob")
+        for be in range(4):
+            mag_a(2, be)
 
         CHAIN_ROUNDS = (((1, 0), (1, 1)), ((2, 0), (2, 1), (3, 0)), ((3, 1), (4, 0), (4, 1)), ((5, 0), (5, 1)))
         LAST_TAGS = ("v", "v", "k", "tr")
@@ -365,9 +478,13 @@ def tile_causalwaveletfieldattentionh_pa_kernel(tc, x, Wkv, bkv, scale_gain, ski
         def period(i):
             for r in range(4):
                 t, hb = r // 2, r % 2
-                if 0 <= i + 1 < 8:
-                    values(i + 1, r)
-                if 4 <= i + 4 < 8:
+                if r == 0 and i == 0:
+                    mag_b(2)
+                    mag_c(2)
+                if i == 0:
+                    keys(3 + r // 2, 2 * (r % 2), "k")
+                    keys(3 + r // 2, 2 * (r % 2) + 1, "ob")
+                elif i + 4 < 8:
                     keys(i + 4, r)
                 if 0 <= i < 8:
                     field_to_tokens(i, t, hb)
@@ -375,19 +492,37 @@ def tile_causalwaveletfieldattentionh_pa_kernel(tc, x, Wkv, bkv, scale_gain, ski
                     toeplitz(i - 1, t, hb, "ob")
                 if 0 <= i - 1 < 8:
                     finish(i - 1, t, hb)
-                if r == 3 and 3 <= i + 3 < 8:
-                    mag_b(i + 3)
-                if 3 <= i + 3 < 8 and r < 3:
-                    mag_a(i + 3, r)
+                if i == 0:
                     if r == 2:
-                        mag_a(i + 3, 3)
+                        for be in range(4):
+                            mag_a(3, be)
+                    if r == 3:
+                        mag_b(3)
+                elif 4 <= i + 3 < 8:
+                    if r == 3:
+                        mag_b(i + 3)
+                    else:
+                        mag_a(i + 3, r)
+                        if r == 2:
+                            mag_a(i + 3, 3)
+                nv = 4 * (i + 1) + r + 1
+                if 5 < nv < 32:
+                    values(nv // 4, nv % 4)
+                if r == 1 and 5 <= i + 5 < 8:
+                    regroup_w(i + 5, False)
+                if r == 0 and 3 <= i + 2 < 8:
+                    regroup_w(8 + i + 2, False)
                 if 0 <= i < 8:
                     for tap, part in CHAIN_ROUNDS[r]:
                         chain(i, tap, part)
+                if r == 2 and 5 <= i + 5 < 8:
+                    quant_w(i + 5)
+                if r == 1 and 3 <= i + 2 < 8:
+                    quant_w(8 + i + 2)
                 if 0 <= i + 1 < 8:
                     field(i + 1, r)
                     first_tap(i + 1, r)
-                if r == 3 and 2 <= i + 3 < 8:
+                if r == 3 and 3 <= i + 3 < 8:
                     mag_c(i + 3)
                 if r == 3 and 0 <= i < 8:
                     skips(i)
@@ -395,43 +530,5 @@ def tile_causalwaveletfieldattentionh_pa_kernel(tc, x, Wkv, bkv, scale_gain, ski
                 for r in range(4):
                     toeplitz(7, r // 2, r % 2, LAST_TAGS[r])
 
-        for j in (1, 2, 3):
-            for be in range(4):
-                keys(j, be, ("k", "ob", "ob", "tr")[be])
-            if j < 3:
-                for be in range(4):
-                    mag_a(j, be)
-            if j < 3:
-                mag_b(j)
-            if j == 1:
-                mag_c(1)
-        fv = fp[:, 0 : NH * 384].rearrange("p (h y) -> p h y", y=384)
-        big = [(0, t0[:])]
-        big += [(2**m, pt[:, m + 3, :]) for m in range(8)]
-        big += [(3 * 2**m, rt[:, m + 3, :]) for m in range(7)]
-        for sig, src in big:
-            for shift, scal in ((0, 1.0), (64, sw[:, 0:1]), (128, sw[:, 1:2])):
-                if sig + shift < NQ:
-                    pos = 128 + sig + shift
-                    nc.vector.scalar_tensor_tensor(
-                        out=fv[:, :, pos : pos + 1],
-                        in0=src.unsqueeze(2),
-                        scalar=scal,
-                        in1=fv[:, :, pos : pos + 1],
-                        op0=ALU.mult,
-                        op1=ALU.add,
-                    )
-        nc.gpsimd.dma_start(
-            out=oflat[TOEP_BASE : TOEP_BASE + P * FROW].rearrange("(p f) -> p f", f=FROW), in_=fp[:]
-        )
-        nc.gpsimd.dma_start(
-            out=wt[:],
-            in_=oflat[TOEP_BASE + 128 : TOEP_BASE + 128 + P * (FROW - 1)].rearrange(
-                "(p h y) -> p h y", h=NH, y=384
-            )[:, :, 0:NQ],
-        )
-        quant_w(wst_b, DM)
-        quant_w(wst_c, 512)
-        quant_w(wst_d, DM + 512)
-        for i in range(-1, 9):
+        for i in range(9):
             period(i)

@@ -26,7 +26,7 @@ FLOPS = 2 * NTOK * DM * 2 * DM
 FROW = NH * 384 + 1
 TOEP_BASE = 9 * NTOK * HD
 MAG_BASE = 15 * NTOK * HD + NTOK * HD // 2
-SMALL_TAPS = ((1, 0), (2, 1), (3, 3), (4, 2), (6, 4), (12, 5))
+SMALL_TAPS = ((1, 0), (2, 1), (3, 3), (4, 2), (12, 5), (6, 4))
 PSB = {"v": 2, "k": 1, "tr": 1, "ob": 2, "sm": 1, "mt": 1}
 
 
@@ -50,7 +50,6 @@ def tile_causalwaveletfieldattentionh_pa_kernel(tc, x, Wkv, bkv, scale_gain, ski
         ident = const.tile([P, P], F32, name="ident")
         make_identity(nc, ident[:])
         fp = ov.tile([P, FROW], F32, name="fp", offset=0)
-        nc.gpsimd.memset(fp[:], 0.0)
         fts = [const.tile([P, NB, HALO + NQ], F32, name="ft%d" % j) for j in range(2)]
         for j in range(2):
             nc.gpsimd.memset(fts[j][:, :, 0:HALO], 0.0)
@@ -66,6 +65,7 @@ def tile_causalwaveletfieldattentionh_pa_kernel(tc, x, Wkv, bkv, scale_gain, ski
         nc.vector.memset(pt[:, 10:11, :], 0.0)
         warm = const.tile([P, 1], F32, name="warm")
         nc.vector.memset(warm[:], 1.0)
+        nc.vector.memset(fp[:].bitcast(mybir.dt.int32), 0)
 
         xc = const.tile([P, 2, NTOK], U32, name="xc", align_bytes=64)
         xsc = const.tile([P, 2, NTOK], U8, name="xsc", align_bytes=64)
@@ -115,11 +115,10 @@ def tile_causalwaveletfieldattentionh_pa_kernel(tc, x, Wkv, bkv, scale_gain, ski
             return xs
 
         st = {}
-        load_w(0, P)
-        xss = [load_x(be) for be in range(4)]
-        load_w(DM, DM + P)
-        load_w(P, 512)
-        load_w(DM + P, DM + 512)
+        xss = [load_x(0)]
+        load_w(0, 512)
+        xss += [load_x(be) for be in range(1, 4)]
+        load_w(DM, DM + 512)
         load_w(512, DM)
         load_w(DM + 512, 2 * DM)
 
@@ -381,7 +380,7 @@ def tile_causalwaveletfieldattentionh_pa_kernel(tc, x, Wkv, bkv, scale_gain, ski
                 out=ut[:, t, :, 4 * hb : 4 * hb + 4, :], in_=ob[:].rearrange("p b (h c) -> p h b c", h=2)
             )
             if hb == 1:
-                nc.gpsimd.dma_start(
+                nc.sync.dma_start(
                     out=oview[:, 2 * i : 2 * i + 2, t : t + 1, :].rearrange("p h o f -> p (h o) f"),
                     in_=ut[:, t].rearrange("p h b c -> p h (b c)"),
                 )

@@ -26,7 +26,7 @@ FLOPS = 2 * NTOK * DM * 2 * DM
 FROW = NH * 384 + 1
 TOEP_BASE = 9 * NTOK * HD
 MAG_BASE = 15 * NTOK * HD + NTOK * HD // 2
-SMALL_TAPS = ((1, 0), (2, 1), (3, 3), (4, 2), (12, 5), (6, 4))
+SMALL_TAPS = ((1, 0), (2, 1), (3, 3), (4, 2), (6, 4), (12, 5))
 PSB = {"v": 2, "k": 1, "tr": 1, "ob": 2, "sm": 1, "mt": 1}
 
 
@@ -40,16 +40,14 @@ def tile_causalwaveletfieldattentionh_pa_kernel(tc, x, Wkv, bkv, scale_gain, ski
     with ExitStack() as ctx:
         const = ctx.enter_context(tc.tile_pool(name="const", bufs=1))
         sh = ctx.enter_context(tc.tile_pool(name="sh", bufs=2))
-        ov = ctx.enter_context(tc.tile_pool(name="ov", bufs=1))
         ps = ctx.enter_context(tc.psum_pool(name="ps", bufs=1))
         ctx.enter_context(tc.manual_schedule())
 
         def slot(shape, dtype, name, tag):
-            return sh.tile(shape, dtype, name=name, tag=tag, bufs=2, align_bytes=64)
+            return sh.tile(shape, dtype, name=name, tag=tag, bufs=(4 if tag == "B" else 2), align_bytes=64)
 
         ident = const.tile([P, P], F32, name="ident")
         make_identity(nc, ident[:])
-        fp = ov.tile([P, FROW], F32, name="fp", offset=0)
         fts = [const.tile([P, NB, HALO + NQ], F32, name="ft%d" % j) for j in range(2)]
         for j in range(2):
             nc.gpsimd.memset(fts[j][:, :, 0:HALO], 0.0)
@@ -65,13 +63,14 @@ def tile_causalwaveletfieldattentionh_pa_kernel(tc, x, Wkv, bkv, scale_gain, ski
         nc.vector.memset(pt[:, 10:11, :], 0.0)
         warm = const.tile([P, 1], F32, name="warm")
         nc.vector.memset(warm[:], 1.0)
-        nc.vector.memset(fp[:].bitcast(mybir.dt.int32), 0)
+        fp = const.tile([P, FROW], F32, name="fp")
+        nc.scalar.activation(out=fp[:, 0:3072], in_=warm[:, 0:1].to_broadcast([P, 3072]), func=ACT.Copy, scale=0.0)
+        nc.vector.memset(fp[:, 3072:FROW], 0.0)
 
         xc = const.tile([P, 2, NTOK], U32, name="xc", align_bytes=64)
         xsc = const.tile([P, 2, NTOK], U8, name="xsc", align_bytes=64)
-        wc = const.tile([P, 16, 2, P], U32, name="wc", align_bytes=64)
-        wsc = const.tile([P, 16, 2, P], U8, name="wsc", align_bytes=64)
-        wraw = const.tile([P, 2, 4, 2 * DM], BF16, name="wraw")
+        wc = const.tile([P, 2, 2 * DM], U32, name="wc", align_bytes=64)
+        wsc = const.tile([P, 2, 2 * DM], U8, name="wsc", align_bytes=64)
         wt = const.tile([P, NH, NQ], F32, name="wt")
         bT = const.tile([P, 16], F32, name="bT")
         csm = const.tile([P, 8, 6], F32, name="csm")
@@ -84,43 +83,42 @@ def tile_causalwaveletfieldattentionh_pa_kernel(tc, x, Wkv, bkv, scale_gain, ski
         bkb = const.tile([16, P], BF16, name="bkb")
         nc.sync.dma_start(out=bkb[:], in_=bkv.rearrange("(m c) -> m c", c=P))
 
-        def load_w(c0, c1):
+        def load_w(c0):
+            wst = slot([P, 2, 4, 512], BF16, "wst", "B")
             for g in range(2):
                 for u in range(2):
                     r0 = 512 * g + 256 * u
                     nc.sync.dma_start(
-                        out=wraw[:, g, 2 * u : 2 * u + 2, c0:c1],
-                        in_=Wkv[r0 : r0 + 256, c0:c1].rearrange("(p e) c -> p e c", e=2),
+                        out=wst[:, g, 2 * u : 2 * u + 2, :],
+                        in_=Wkv[r0 : r0 + 256, c0 : c0 + 512].rearrange("(p e) c -> p e c", e=2),
                     )
+            return wst
 
-        def regroup_w(m, on_vector):
-            wg = sh.tile([P, 2, P, 4], BF16, name="wg", bufs=3, align_bytes=64)
-            st["wg", m] = wg
-            src = wraw[:, :, :, P * m : P * m + P].rearrange("p g t c -> p g c t")
-            if on_vector:
-                nc.vector.tensor_copy(out=wg[:], in_=src)
-            else:
-                nc.scalar.copy(out=wg[:], in_=src)
-
-        def quant_w(m):
-            nc.vector.quantize_mx(
-                out=wc[:, m].rearrange("p g c -> p (g c)").bitcast(FP8X4),
-                scales=wsc[:, m].rearrange("p g c -> p (g c)"),
-                in_=st["wg", m][:].rearrange("p g c t -> p (g c t)"),
-            )
+        def quant_w(wst, c0):
+            wg = slot([P, 2, 512, 4], BF16, "wg", "D")
+            for g in range(2):
+                nc.vector.tensor_copy(
+                    out=wg[:, g].rearrange("p (c i) t -> p c t i", i=4),
+                    in_=wst[:, g].rearrange("p t (c i) -> p c t i", i=4),
+                )
+            for g in range(2):
+                nc.vector.quantize_mx(
+                    out=wc[:, g, c0 : c0 + 512].bitcast(FP8X4),
+                    scales=wsc[:, g, c0 : c0 + 512],
+                    in_=wg[:, g].rearrange("p c t -> p (c t)"),
+                )
 
         def load_x(be):
             xs = slot([P, 2, 2, DM], BF16, "xs", "AE"[be % 2])
             nc.sync.dma_start(out=xs[:], in_=xview[:, :, 2 * be : 2 * be + 2, :])
             return xs
 
-        st = {}
         xss = [load_x(0)]
-        load_w(0, 512)
+        wst_a = load_w(0)
         xss += [load_x(be) for be in range(1, 4)]
-        load_w(DM, DM + 512)
-        load_w(512, DM)
-        load_w(DM + 512, 2 * DM)
+        wst_b = load_w(DM)
+        wst_c = load_w(512)
+        wst_d = load_w(DM + 512)
 
         sg = const.tile([P, 10, NH], F32, name="sg")
         nc.vector.tensor_copy(out=sg[:].rearrange("p j h -> p (j h)"), in_=sgb[:])
@@ -133,14 +131,11 @@ def tile_causalwaveletfieldattentionh_pa_kernel(tc, x, Wkv, bkv, scale_gain, ski
         nc.scalar.activation(out=eg[:], in_=sg[:], func=ACT.Exp)
         skf = const.tile([P, 2], F32, name="skf")
         nc.vector.tensor_copy(out=skf[:], in_=skb[:])
-        nc.scalar.activation(out=skf[:], in_=skf[:], func=ACT.Exp, scale=-1.0)
-        nc.scalar.activation(out=warm[:], in_=warm[:], func=ACT.Sqrt)
+        nc.scalar.activation(out=sw[:], in_=skf[:], func=ACT.Sigmoid)
         nc.vector.tensor_copy(out=bkf[0:16, :], in_=bkb[:])
         bps = ps.tile([P, P], F32, name="bps", tag="sm")
         nc.tensor.transpose(bps[:], bkf[:], ident[:])
         nc.vector.tensor_copy(out=bT[:], in_=bps[:, 0:16])
-        regroup_w(0, True)
-        quant_w(0)
 
         ssum = const.tile([P, NH], F32, name="ssum")
         nc.vector.tensor_reduce(out=ssum[:], in_=eg[:].rearrange("p j h -> p h j"), axis=AX.X, op=ALU.add)
@@ -159,8 +154,6 @@ def tile_causalwaveletfieldattentionh_pa_kernel(tc, x, Wkv, bkv, scale_gain, ski
         t0 = const.tile([P, NH], F32, name="t0")
         nc.vector.tensor_reduce(out=t0[:], in_=gn[:].rearrange("p j h -> p h j"), axis=AX.X, op=ALU.add)
         nc.vector.tensor_scalar_mul(out=t0[:], in0=t0[:], scalar1=d3)
-        nc.vector.tensor_scalar_add(out=skf[:], in0=skf[:], scalar1=1.0)
-        nc.vector.reciprocal(out=sw[:], in_=skf[:])
         for hh in range(2):
             lo = 64 * hh
             nc.vector.tensor_copy(
@@ -170,46 +163,17 @@ def tile_causalwaveletfieldattentionh_pa_kernel(tc, x, Wkv, bkv, scale_gain, ski
                 out=csm[lo : lo + 64, :, 3:6], in_=rt[lo : lo + 64, 0:3, hh:NH:2].rearrange("p r i -> p i r")
             )
 
-        big = [(0, t0[:])]
-        big += [(2**m, pt[:, m + 3, :]) for m in range(8)]
-        big += [(3 * 2**m, rt[:, m + 3, :]) for m in range(7)]
-        toep_ops = []
-        for sig, src in big:
-            for shift, scal in ((0, 1.0), (64, sw[:, 0:1]), (128, sw[:, 1:2])):
-                if sig + shift < NQ:
-                    toep_ops.append((128 + sig + shift, src, scal))
+        quant_w(wst_a, 0)
 
-        fv = fp[:, 0 : NH * 384].rearrange("p (h y) -> p h y", y=384)
-
-        def toep_fill(lo, hi):
-            for pos, src, scal in toep_ops[lo:hi]:
-                nc.vector.scalar_tensor_tensor(
-                    out=fv[:, :, pos : pos + 1],
-                    in0=src.unsqueeze(2),
-                    scalar=scal,
-                    in1=fv[:, :, pos : pos + 1],
-                    op0=ALU.mult,
-                    op1=ALU.add,
-                )
-
-        def toep_dma():
-            nc.gpsimd.dma_start(
-                out=oflat[TOEP_BASE : TOEP_BASE + P * FROW].rearrange("(p f) -> p f", f=FROW), in_=fp[:]
-            )
-            nc.gpsimd.dma_start(
-                out=wt[:],
-                in_=oflat[TOEP_BASE + 128 : TOEP_BASE + 128 + P * (FROW - 1)].rearrange(
-                    "(p h y) -> p h y", h=NH, y=384
-                )[:, :, 0:NQ],
-            )
+        st = {}
 
         def mx_group(m, be, tag):
             acc = ps.tile([P, 512], F32, name="acc", tag=tag, bufs=PSB[tag])
             for g in range(2):
                 nc.tensor.matmul_mx(
                     out=acc[:],
-                    lhsT=wc[:, m, g, :].bitcast(FP8X4),
-                    lhsT_scale=wsc[:, m, g, :],
+                    lhsT=wc[:, g, P * m : P * m + P].bitcast(FP8X4),
+                    lhsT_scale=wsc[:, g, P * m : P * m + P],
                     rhs=xc[:, g, 512 * be : 512 * be + 512].bitcast(FP8X4),
                     rhs_scale=xsc[:, g, 512 * be : 512 * be + 512],
                     start=(g == 0),
@@ -234,29 +198,8 @@ def tile_causalwaveletfieldattentionh_pa_kernel(tc, x, Wkv, bkv, scale_gain, ski
                 nc.tensor.matmul(
                     out=msq[:, j:32:16], lhsT=ksq[:, P * j : P * j + P], rhs=ind[:], start=True, stop=True
                 )
-            if be == 3 and i >= 2:
+            if be == 3:
                 nc.scalar.activation(out=magt[:, 0:32], in_=msq[:], func=ACT.Sqrt)
-
-        def mag_r(i, be):
-            rep = sh.tile([P, 4, P], F32, name="rep", bufs=2)
-            st["rep", i, be] = rep
-            src = st["msq", i][:].rearrange("p (h j) -> p j h", h=2)[:, 4 * be : 4 * be + 4, :]
-            nc.scalar.activation(
-                out=rep[:].rearrange("p j (h c) -> p j h c", h=2),
-                in_=src.unsqueeze(3).to_broadcast([P, 4, 2, HD]),
-                func=ACT.Sqrt,
-            )
-
-        def mag_t(i, be, tag):
-            if be == 0:
-                st["magbc", i] = slot([P, NTOK], F32, "magbc", "E")
-            rep = st["rep", i, be]
-            bank = ps.tile([P, 4, P], F32, name="mbank", tag=tag, bufs=PSB[tag])
-            for j4 in range(4):
-                nc.tensor.transpose(bank[:, j4, :], rep[:, j4, :], ident[:])
-            nc.scalar.copy(
-                out=st["magbc", i][:, 512 * be : 512 * be + 512], in_=bank[:].rearrange("p j t -> p (j t)")
-            )
 
         def mag_b(i):
             mtp = ps.tile([P, P], F32, name="mtp", tag="mt")
@@ -321,7 +264,7 @@ def tile_causalwaveletfieldattentionh_pa_kernel(tc, x, Wkv, bkv, scale_gain, ski
 
         def skips(i):
             u = st["u", i]
-            up = ov.tile([P, NB, NQ], F32, name="up", tag="up", bufs=2, offset=16384)
+            up = slot([P, NB, NQ], F32, "up", "B")
             st["up", i] = up
             nc.scalar.copy(out=up[:, :, 0:64], in_=u[:, :, 0:64])
             nc.vector.scalar_tensor_tensor(
@@ -369,7 +312,7 @@ def tile_causalwaveletfieldattentionh_pa_kernel(tc, x, Wkv, bkv, scale_gain, ski
             up = st["up", i]
             ob = st["ob", i, t, hb]
             if t == 0 and hb == 0:
-                st["ut", i] = ov.tile([P, 2, 2, NB, HD], F32, name="ut", tag="ut", bufs=2, offset=0)
+                st["ut", i] = slot([P, 2, 2, NB, HD], F32, "ut", "D")
             ut = st["ut", i]
             for b4 in range(4):
                 nc.tensor.matmul(
@@ -385,7 +328,7 @@ def tile_causalwaveletfieldattentionh_pa_kernel(tc, x, Wkv, bkv, scale_gain, ski
                     in_=ut[:, t].rearrange("p h b c -> p h (b c)"),
                 )
 
-        def x_chunk(be):
+        for be in range(4):
             xs = xss[be]
             xg = slot([P, 2, 512, 4], BF16, "xg", "C")
             xg32 = xg[:].bitcast(F32)
@@ -404,72 +347,24 @@ def tile_causalwaveletfieldattentionh_pa_kernel(tc, x, Wkv, bkv, scale_gain, ski
                         nc.vector.tensor_copy(out=dst, in_=src)
                     else:
                         nc.scalar.copy(out=dst, in_=src)
-            return xg
-
-        def x_quant(be, xg):
+            if be >= 1:
+                keys(0, be - 1, "kv"[be % 2])
+            if be >= 2:
+                mag_a(0, be - 2)
             for g in range(2):
                 nc.vector.quantize_mx(
                     out=xc[:, g, 512 * be : 512 * be + 512].bitcast(FP8X4),
                     scales=xsc[:, g, 512 * be : 512 * be + 512],
                     in_=xg[:, g].rearrange("p c j -> p (c j)"),
                 )
-
-        for it in range(7):
-            if it < 4:
-                xg = x_chunk(it)
-            if 1 <= it <= 4:
-                keys(0, it - 1, "k")
-            if 2 <= it <= 5:
-                mag_a(0, it - 2)
-                mag_r(0, it - 2)
-            if 3 <= it <= 6:
-                mag_t(0, it - 3, "v")
-            if it < 4:
-                x_quant(it, xg)
-                toep_fill(12 * it, 12 * it + 12)
-            if it == 3:
-                toep_dma()
-            if it == 4:
-                regroup_w(8, True)
-                quant_w(8)
-                regroup_w(1, True)
-                quant_w(1)
-            if it >= 4:
-                keys(1, it - 4, ("ob", "ob", "tr")[it - 4])
+        keys(0, 3, "k")
+        mag_a(0, 2)
+        mag_a(0, 3)
+        mag_b(0)
+        mag_c(0)
+        quant_w(wst_b, DM)
         values(0, 0)
-        keys(1, 3, "mt")
         values(0, 1)
-        for m in (9, 2, 3, 4, 10):
-            regroup_w(m, True)
-            quant_w(m)
-        field(0, 0)
-        first_tap(0, 0)
-        values(0, 2)
-        field(0, 1)
-        first_tap(0, 1)
-        values(0, 3)
-        for be in range(4):
-            mag_a(1, be)
-        field(0, 2)
-        first_tap(0, 2)
-        values(1, 0)
-        field(0, 3)
-        first_tap(0, 3)
-        values(1, 1)
-        mag_r(1, 0)
-        mag_r(1, 1)
-        mag_t(1, 0, "ob")
-        keys(2, 0, "k")
-        mag_r(1, 2)
-        mag_t(1, 1, "ob")
-        keys(2, 1, "tr")
-        mag_r(1, 3)
-        mag_t(1, 2, "ob")
-        keys(2, 2, "mt")
-        keys(2, 3, "k")
-        mag_t(1, 3, "ob")
-        for be in range(4):
-            mag_a(2, be)
 
         CHAIN_ROUNDS = (((1, 0), (1, 1)), ((2, 0), (2, 1), (3, 0)), ((3, 1), (4, 0), (4, 1)), ((5, 0), (5, 1)))
         LAST_TAGS = ("v", "v", "k", "tr")
@@ -477,13 +372,9 @@ def tile_causalwaveletfieldattentionh_pa_kernel(tc, x, Wkv, bkv, scale_gain, ski
         def period(i):
             for r in range(4):
                 t, hb = r // 2, r % 2
-                if r == 0 and i == 0:
-                    mag_b(2)
-                    mag_c(2)
-                if i == 0:
-                    keys(3 + r // 2, 2 * (r % 2), "k")
-                    keys(3 + r // 2, 2 * (r % 2) + 1, "ob")
-                elif i + 4 < 8:
+                if 0 <= i + 1 < 8 and (i >= 0 or r >= 2):
+                    values(i + 1, r)
+                if 4 <= i + 4 < 8:
                     keys(i + 4, r)
                 if 0 <= i < 8:
                     field_to_tokens(i, t, hb)
@@ -491,37 +382,19 @@ def tile_causalwaveletfieldattentionh_pa_kernel(tc, x, Wkv, bkv, scale_gain, ski
                     toeplitz(i - 1, t, hb, "ob")
                 if 0 <= i - 1 < 8:
                     finish(i - 1, t, hb)
-                if i == 0:
+                if r == 3 and 3 <= i + 3 < 8:
+                    mag_b(i + 3)
+                if 3 <= i + 3 < 8 and r < 3:
+                    mag_a(i + 3, r)
                     if r == 2:
-                        for be in range(4):
-                            mag_a(3, be)
-                    if r == 3:
-                        mag_b(3)
-                elif 4 <= i + 3 < 8:
-                    if r == 3:
-                        mag_b(i + 3)
-                    else:
-                        mag_a(i + 3, r)
-                        if r == 2:
-                            mag_a(i + 3, 3)
-                nv = 4 * (i + 1) + r + 1
-                if 5 < nv < 32:
-                    values(nv // 4, nv % 4)
-                if r == 1 and 5 <= i + 5 < 8:
-                    regroup_w(i + 5, False)
-                if r == 0 and 3 <= i + 2 < 8:
-                    regroup_w(8 + i + 2, False)
+                        mag_a(i + 3, 3)
                 if 0 <= i < 8:
                     for tap, part in CHAIN_ROUNDS[r]:
                         chain(i, tap, part)
-                if r == 2 and 5 <= i + 5 < 8:
-                    quant_w(i + 5)
-                if r == 1 and 3 <= i + 2 < 8:
-                    quant_w(8 + i + 2)
                 if 0 <= i + 1 < 8:
                     field(i + 1, r)
                     first_tap(i + 1, r)
-                if r == 3 and 3 <= i + 3 < 8:
+                if r == 3 and 2 <= i + 3 < 8:
                     mag_c(i + 3)
                 if r == 3 and 0 <= i < 8:
                     skips(i)
@@ -529,5 +402,42 @@ def tile_causalwaveletfieldattentionh_pa_kernel(tc, x, Wkv, bkv, scale_gain, ski
                 for r in range(4):
                     toeplitz(7, r // 2, r % 2, LAST_TAGS[r])
 
-        for i in range(9):
+        for j in (1, 2, 3):
+            for be in range(4):
+                keys(j, be, ("k", "ob", "ob", "tr")[be])
+            if j < 3:
+                for be in range(4):
+                    mag_a(j, be)
+            if j < 3:
+                mag_b(j)
+            if j == 1:
+                mag_c(1)
+        fv = fp[:, 0 : NH * 384].rearrange("p (h y) -> p h y", y=384)
+        big = [(0, t0[:])]
+        big += [(2**m, pt[:, m + 3, :]) for m in range(8)]
+        big += [(3 * 2**m, rt[:, m + 3, :]) for m in range(7)]
+        for sig, src in big:
+            for shift, scal in ((0, 1.0), (64, sw[:, 0:1]), (128, sw[:, 1:2])):
+                if sig + shift < NQ:
+                    pos = 128 + sig + shift
+                    nc.vector.scalar_tensor_tensor(
+                        out=fv[:, :, pos : pos + 1],
+                        in0=src.unsqueeze(2),
+                        scalar=scal,
+                        in1=fv[:, :, pos : pos + 1],
+                        op0=ALU.mult,
+                        op1=ALU.add,
+                    )
+        nc.sync.dma_start(
+            out=oflat[TOEP_BASE : TOEP_BASE + P * FROW].rearrange("(p f) -> p f", f=FROW), in_=fp[:]
+        )
+        nc.sync.dma_start(
+            out=wt[:],
+            in_=oflat[TOEP_BASE + 128 : TOEP_BASE + 128 + P * (FROW - 1)].rearrange(
+                "(p h y) -> p h y", h=NH, y=384
+            )[:, :, 0:NQ],
+        )
+        quant_w(wst_c, 512)
+        quant_w(wst_d, DM + 512)
+        for i in range(-1, 9):
             period(i)

@@ -365,6 +365,14 @@ def tile_causalwaveletfieldattentionh_pa_kernel(tc, x, Wkv, bkv, scale_gain, ski
         quant_w(wst_b, DM)
         values(0, 0)
         values(0, 1)
+        for be in range(4):
+            keys(1, be, ("k", "ob", "ob", "tr")[be])
+        for be in range(4):
+            mag_a(1, be)
+        for be in range(4):
+            keys(2, be, ("k", "ob", "ob", "tr")[be])
+        mag_b(1)
+        mag_c(1)
 
         CHAIN_ROUNDS = (((1, 0), (1, 1)), ((2, 0), (2, 1), (3, 0)), ((3, 1), (4, 0), (4, 1)), ((5, 0), (5, 1)))
         LAST_TAGS = ("v", "v", "k", "tr")
@@ -374,7 +382,10 @@ def tile_causalwaveletfieldattentionh_pa_kernel(tc, x, Wkv, bkv, scale_gain, ski
                 t, hb = r // 2, r % 2
                 if 0 <= i + 1 < 8 and (i >= 0 or r >= 2):
                     values(i + 1, r)
-                if 4 <= i + 4 < 8:
+                if i == 0:
+                    keys(3 + r // 2, 2 * (r % 2), "k")
+                    keys(3 + r // 2, 2 * (r % 2) + 1, "ob")
+                elif 5 <= i + 4 < 8:
                     keys(i + 4, r)
                 if 0 <= i < 8:
                     field_to_tokens(i, t, hb)
@@ -384,7 +395,14 @@ def tile_causalwaveletfieldattentionh_pa_kernel(tc, x, Wkv, bkv, scale_gain, ski
                     finish(i - 1, t, hb)
                 if r == 3 and 3 <= i + 3 < 8:
                     mag_b(i + 3)
-                if 3 <= i + 3 < 8 and r < 3:
+                if i == 0:
+                    if r == 0 or r == 2:
+                        for be in range(4):
+                            mag_a(2 + r // 2, be)
+                    if r == 1:
+                        mag_b(2)
+                        mag_c(2)
+                if 4 <= i + 3 < 8 and r < 3:
                     mag_a(i + 3, r)
                     if r == 2:
                         mag_a(i + 3, 3)
@@ -394,7 +412,7 @@ def tile_causalwaveletfieldattentionh_pa_kernel(tc, x, Wkv, bkv, scale_gain, ski
                 if 0 <= i + 1 < 8:
                     field(i + 1, r)
                     first_tap(i + 1, r)
-                if r == 3 and 2 <= i + 3 < 8:
+                if r == 3 and 3 <= i + 3 < 8:
                     mag_c(i + 3)
                 if r == 3 and 0 <= i < 8:
                     skips(i)
@@ -402,16 +420,6 @@ def tile_causalwaveletfieldattentionh_pa_kernel(tc, x, Wkv, bkv, scale_gain, ski
                 for r in range(4):
                     toeplitz(7, r // 2, r % 2, LAST_TAGS[r])
 
-        for j in (1, 2, 3):
-            for be in range(4):
-                keys(j, be, ("k", "ob", "ob", "tr")[be])
-            if j < 3:
-                for be in range(4):
-                    mag_a(j, be)
-            if j < 3:
-                mag_b(j)
-            if j == 1:
-                mag_c(1)
         fv = fp[:, 0 : NH * 384].rearrange("p (h y) -> p h y", y=384)
         big = [(0, t0[:])]
         big += [(2**m, pt[:, m + 3, :]) for m in range(8)]

from contextlib import ExitStack

import concourse.mybir as mybir
from concourse.masks import make_identity

F32 = mybir.dt.float32
BF16 = mybir.dt.bfloat16
U32 = mybir.dt.uint32
U8 = mybir.dt.uint8
FP8X4 = mybir.dt.float8_e4m3fn_x4
ALU = mybir.AluOpType
ACT = mybir.ActivationFunctionType
AX = mybir.AxisListType

P = 128
NTOK = 2048
DM = 1024
NH = 16
HD = 64
NB = 8
NQ = 256
HALO = 8
D4 = (0.4829629131445341, 0.8365163037378079, 0.2241438680420134, -0.1294095225512604)
FLOPS = 2 * NTOK * DM * 2 * DM

FROW = NH * 384 + 1
TOEP_BASE = 9 * NTOK * HD
MAG_BASE = 15 * NTOK * HD + NTOK * HD // 2
SMALL_TAPS = ((1, 0), (2, 1), (3, 3), (4, 2), (6, 4), (12, 5))
PSB = {"v": 2, "k": 1, "tr": 1, "ob": 2, "sm": 1, "mt": 1}


def tile_causalwaveletfieldattentionh_pa_kernel(tc, x, Wkv, bkv, scale_gain, skip_w, out):
    nc = tc.nc
    d0, d1, d2, d3 = D4
    oflat = out.rearrange("o h n c -> (o h n c)")
    oview = out.rearrange("o h (t p b) c -> p (o h) t (b c)", t=2, p=P, b=NB)
    xview = x.rearrange("o (t p b) k -> p (o t) b k", t=2, p=P, b=NB)

    with ExitStack() as ctx:
        const = ctx.enter_context(tc.tile_pool(name="const", bufs=1))
        sh = ctx.enter_context(tc.tile_pool(name="sh", bufs=2))
        ps = ctx.enter_context(tc.psum_pool(name="ps", bufs=1))
        ctx.enter_context(tc.manual_schedule())

        def slot(shape, dtype, name, tag):
            return sh.tile(shape, dtype, name=name, tag=tag, bufs=(4 if tag == "B" else 2), align_bytes=64)

        ident = const.tile([P, P], F32, name="ident")
        make_identity(nc, ident[:])
        fts = [const.tile([P, NB, HALO + NQ], F32, name="ft%d" % j) for j in range(2)]
        for j in range(2):
            nc.gpsimd.memset(fts[j][:, :, 0:HALO], 0.0)
        ind = const.tile([P, 2], F32, name="ind")
        nc.vector.memset(ind[:], 0.0)
        nc.vector.memset(ind[0:64, 0:1], 1.0)
        nc.vector.memset(ind[64:128, 1:2], 1.0)
        magt = const.tile([P, P], F32, name="magt")
        nc.vector.memset(magt[:], 0.0)
        bkf = const.tile([P, P], F32, name="bkf")
        nc.vector.memset(bkf[:], 0.0)
        pt = const.tile([P, 11, NH], F32, name="pt")
        nc.vector.memset(pt[:, 10:11, :], 0.0)
        warm = const.tile([P, 1], F32, name="warm")
        nc.vector.memset(warm[:], 1.0)
        fp = const.tile([P, FROW], F32, name="fp")
        nc.scalar.activation(out=fp[:, 0:3072], in_=warm[:, 0:1].to_broadcast([P, 3072]), func=ACT.Copy, scale=0.0)
        nc.vector.memset(fp[:, 3072:FROW], 0.0)

        xc = const.tile([P, 2, NTOK], U32, name="xc", align_bytes=64)
        xsc = const.tile([P, 2, NTOK], U8, name="xsc", align_bytes=64)
        wc = const.tile([P, 2, 2 * DM], U32, name="wc", align_bytes=64)
        wsc = const.tile([P, 2, 2 * DM], U8, name="wsc", align_bytes=64)
        wt = const.tile([P, NH, NQ], F32, name="wt")
        bT = const.tile([P, 16], F32, name="bT")
        csm = const.tile([P, 8, 6], F32, name="csm")
        sw = const.tile([P, 2], F32, name="sw")

        sgb = const.tile([P, 160], BF16, name="sgb")
        nc.sync.dma_start(out=sgb[:], in_=scale_gain.rearrange("j h -> (j h)").partition_broadcast(P))
        skb = const.tile([P, 2], BF16, name="skb")
        nc.sync.dma_start(out=skb[:], in_=skip_w.partition_broadcast(P))
        bkb = const.tile([16, P], BF16, name="bkb")
        nc.sync.dma_start(out=bkb[:], in_=bkv.rearrange("(m c) -> m c", c=P))

        def load_w(c0):
            wst = slot([P, 2, 4, 512], BF16, "wst", "B")
            for g in range(2):
                for u in range(2):
                    r0 = 512 * g + 256 * u
                    nc.sync.dma_start(
                        out=wst[:, g, 2 * u : 2 * u + 2, :],
                        in_=Wkv[r0 : r0 + 256, c0 : c0 + 512].rearrange("(p e) c -> p e c", e=2),
                    )
            return wst

        def quant_w(wst, c0):
            wg = slot([P, 2, 512, 4], BF16, "wg", "D")
            for g in range(2):
                nc.vector.tensor_copy(
                    out=wg[:, g].rearrange("p (c i) t -> p c t i", i=4),
                    in_=wst[:, g].rearrange("p t (c i) -> p c t i", i=4),
                )
            for g in range(2):
                nc.vector.quantize_mx(
                    out=wc[:, g, c0 : c0 + 512].bitcast(FP8X4),
                    scales=wsc[:, g, c0 : c0 + 512],
                    in_=wg[:, g].rearrange("p c t -> p (c t)"),
                )

        def load_x(be):
            xs = slot([P, 2, 2, DM], BF16, "xs", "AE"[be % 2])
            nc.sync.dma_start(out=xs[:], in_=xview[:, :, 2 * be : 2 * be + 2, :])
            return xs

        xss = [load_x(0)]
        wst_a = load_w(0)
        xss += [load_x(be) for be in range(1, 4)]
        wst_b = load_w(DM)
        wst_c = load_w(512)
        wst_d = load_w(DM + 512)

        sg = const.tile([P, 10, NH], F32, name="sg")
        nc.vector.tensor_copy(out=sg[:].rearrange("p j h -> p (j h)"), in_=sgb[:])
        mxg = const.tile([P, NH], F32, name="mxg")
        nc.vector.tensor_reduce(out=mxg[:], in_=sg[:].rearrange("p j h -> p h j"), axis=AX.X, op=ALU.max)
        nc.vector.tensor_tensor(
            out=sg[:], in0=sg[:], in1=mxg[:].unsqueeze(1).to_broadcast([P, 10, NH]), op=ALU.subtract
        )
        eg = const.tile([P, 10, NH], F32, name="eg")
        nc.scalar.activation(out=eg[:], in_=sg[:], func=ACT.Exp)
        skf = const.tile([P, 2], F32, name="skf")
        nc.vector.tensor_copy(out=skf[:], in_=skb[:])
        nc.scalar.activation(out=sw[:], in_=skf[:], func=ACT.Sigmoid)
        nc.vector.tensor_copy(out=bkf[0:16, :], in_=bkb[:])
        bps = ps.tile([P, P], F32, name="bps", tag="sm")
        nc.tensor.transpose(bps[:], bkf[:], ident[:])
        nc.vector.tensor_copy(out=bT[:], in_=bps[:, 0:16])

        ssum = const.tile([P, NH], F32, name="ssum")
        nc.vector.tensor_reduce(out=ssum[:], in_=eg[:].rearrange("p j h -> p h j"), axis=AX.X, op=ALU.add)
        rsum = const.tile([P, NH], F32, name="rsum")
        nc.vector.reciprocal(out=rsum[:], in_=ssum[:])
        gn = const.tile([P, 10, NH], F32, name="gn")
        nc.vector.tensor_tensor(
            out=gn[:], in0=eg[:], in1=rsum[:].unsqueeze(1).to_broadcast([P, 10, NH]), op=ALU.mult
        )
        nc.vector.tensor_scalar_mul(out=pt[:, 0:10, :], in0=gn[:], scalar1=d2)
        nc.vector.scalar_tensor_tensor(
            out=pt[:, 1:11, :], in0=gn[:], scalar=d1, in1=pt[:, 1:11, :], op0=ALU.mult, op1=ALU.add
        )
        rt = const.tile([P, 10, NH], F32, name="rt")
        nc.vector.tensor_scalar_mul(out=rt[:], in0=gn[:], scalar1=d0)
        t0 = const.tile([P, NH], F32, name="t0")
        nc.vector.tensor_reduce(out=t0[:], in_=gn[:].rearrange("p j h -> p h j"), axis=AX.X, op=ALU.add)
        nc.vector.tensor_scalar_mul(out=t0[:], in0=t0[:], scalar1=d3)
        for hh in range(2):
            lo = 64 * hh
            nc.vector.tensor_copy(
                out=csm[lo : lo + 64, :, 0:3], in_=pt[lo : lo + 64, 0:3, hh:NH:2].rearrange("p r i -> p i r")
            )
            nc.vector.tensor_copy(
                out=csm[lo : lo + 64, :, 3:6], in_=rt[lo : lo + 64, 0:3, hh:NH:2].rearrange("p r i -> p i r")
            )

        quant_w(wst_a, 0)

        st = {}

        def mx_group(m, be, tag):
            acc = ps.tile([P, 512], F32, name="acc", tag=tag, bufs=PSB[tag])
            for g in range(2):
                nc.tensor.matmul_mx(
                    out=acc[:],
                    lhsT=wc[:, g, P * m : P * m + P].bitcast(FP8X4),
                    lhsT_scale=wsc[:, g, P * m : P * m + P],
                    rhs=xc[:, g, 512 * be : 512 * be + 512].bitcast(FP8X4),
                    rhs_scale=xsc[:, g, 512 * be : 512 * be + 512],
                    start=(g == 0),
                    stop=(g == 1),
                )
            return acc

        def keys(i, be, tag="k"):
            if be == 0:
                st["ksq", i] = slot([P, NTOK], F32, "ksq", "A")
            acc = mx_group(i, be, tag)
            nc.scalar.activation(
                out=st["ksq", i][:, 512 * be : 512 * be + 512], in_=acc[:], func=ACT.Square, bias=bT[:, i : i + 1]
            )

        def mag_a(i, be):
            ksq = st["ksq", i]
            if be == 0:
                st["msq", i] = ps.tile([P, 32], F32, name="msq", tag="sm")
            msq = st["msq", i]
            for j in range(4 * be, 4 * be + 4):
                nc.tensor.matmul(
                    out=msq[:, j:32:16], lhsT=ksq[:, P * j : P * j + P], rhs=ind[:], start=True, stop=True
                )
            if be == 3:
                nc.scalar.activation(out=magt[:, 0:32], in_=msq[:], func=ACT.Sqrt)

        def mag_b(i):
            mtp = ps.tile([P, P], F32, name="mtp", tag="mt")
            nc.tensor.transpose(mtp[:], magt[:], ident[:])
            mrow = sh.tile([32, P], F32, name="mrow")
            nc.scalar.copy(out=mrow[:], in_=mtp[0:32, :])
            mb = MAG_BASE + 4096 * i
            nc.scalar.dma_start(out=oflat[mb : mb + 4096].rearrange("(r p) -> r p", p=P), in_=mrow[:])

        def mag_c(i):
            mb = MAG_BASE + 4096 * i
            magbc = slot([P, NTOK], F32, "magbc", "E")
            st["magbc", i] = magbc
            for hh in range(2):
                nc.sync.dma_start(
                    out=magbc[64 * hh : 64 * hh + 64, :],
                    in_=oflat[mb + NTOK * hh : mb + NTOK * hh + NTOK].partition_broadcast(64),
                )

        def values(i, be):
            st["v", i, be] = mx_group(8 + i, be, "v")

        def field(i, be):
            nc.vector.scalar_tensor_tensor(
                out=fts[i % 2][:, 2 * be : 2 * be + 2, HALO : HALO + NQ],
                in0=st["v", i, be][:].rearrange("p (b q) -> p b q", b=2),
                scalar=bT[:, 8 + i : 9 + i],
                in1=st["magbc", i][:, 512 * be : 512 * be + 512].rearrange("p (b q) -> p b q", b=2),
                op0=ALU.add,
                op1=ALU.mult,
            )

        def first_tap(i, be):
            ft = fts[i % 2]
            if be == 0:
                st["u", i] = slot([P, NB, NQ], F32, "u", "B")
            u = st["u", i]
            coef = csm[:, i, 0:1]
            if be < 3:
                nc.scalar.activation(
                    out=u[:, 2 * be + 1 : 2 * be + 3, :], in_=ft[:, 2 * be : 2 * be + 2, HALO : HALO + NQ],
                    func=ACT.Copy, scale=coef,
                )
            else:
                nc.scalar.activation(out=u[:, 7:8, :], in_=ft[:, 6:7, HALO : HALO + NQ], func=ACT.Copy, scale=coef)
                nc.scalar.activation(
                    out=u[:, 0:1, :], in_=ft[:, 7:8, HALO - 1 : HALO - 1 + NQ], func=ACT.Copy, scale=coef
                )

        def chain(i, tap, part):
            ft = fts[i % 2]
            u = st["u", i]
            r, ci = SMALL_TAPS[tap]
            rr, ex = r % NB, r // NB
            if part == 0:
                dst, src = u[:, rr:NB, :], ft[:, 0 : NB - rr, HALO - ex : HALO - ex + NQ]
            else:
                dst, src = u[:, 0:rr, :], ft[:, NB - rr : NB, HALO - 1 - ex : HALO - 1 - ex + NQ]
            nc.vector.scalar_tensor_tensor(
                out=dst, in0=src, scalar=csm[:, i, ci : ci + 1], in1=dst, op0=ALU.mult, op1=ALU.add
            )

        def skips(i):
            u = st["u", i]
            up = slot([P, NB, NQ], F32, "up", "B")
            st["up", i] = up
            nc.scalar.copy(out=up[:, :, 0:64], in_=u[:, :, 0:64])
            nc.vector.scalar_tensor_tensor(
                out=up[:, :, 64:256], in0=u[:, :, 0:192], scalar=sw[:, 0:1], in1=u[:, :, 64:256],
                op0=ALU.mult, op1=ALU.add,
            )
            nc.vector.scalar_tensor_tensor(
                out=up[:, :, 128:256], in0=u[:, :, 0:128], scalar=sw[:, 1:2], in1=up[:, :, 128:256],
                op0=ALU.mult, op1=ALU.add,
            )

        def field_to_tokens(i, t, hb):
            ft = fts[i % 2]
            if t == 0 and hb == 0:
                st["ftok", i] = slot([P, 2, 2, NB, HD], F32, "ftok", "C")
            ftok = st["ftok", i]
            bank = ps.tile([P, 4, P], F32, name="bank", tag="tr", bufs=PSB["tr"])
            for b4 in range(4):
                c0 = HALO + P * t
                nc.tensor.transpose(bank[:, b4, :], ft[:, 4 * hb + b4, c0 : c0 + P], ident[:])
            nc.scalar.copy(
                out=ftok[:, t, :, 4 * hb : 4 * hb + 4, :],
                in_=bank[:].rearrange("p b (h c) -> p h b c", h=2),
            )

        def toeplitz(i, t, hb, tag):
            ftok = st["ftok", i]
            ob = ps.tile([P, 4, P], F32, name="ob", tag=tag, bufs=PSB[tag])
            st["ob", i, t, hb] = ob
            first = True
            for hh in range(2):
                h = 2 * i + hh
                for tin in range(t + 1):
                    j0 = P * (t - tin)
                    nc.tensor.matmul(
                        out=ob[:, :, HD * hh : HD * hh + HD],
                        lhsT=wt[:, h, j0 : j0 + P],
                        rhs=ftok[:, tin, hh, 4 * hb : 4 * hb + 4, :],
                        start=first,
                        stop=False,
                    )
                    first = False

        def finish(i, t, hb):
            up = st["up", i]
            ob = st["ob", i, t, hb]
            if t == 0 and hb == 0:
                st["ut", i] = slot([P, 2, 2, NB, HD], F32, "ut", "D")
            ut = st["ut", i]
            for b4 in range(4):
                nc.tensor.matmul(
                    out=ob[:, b4, :], lhsT=up[:, 4 * hb + b4, P * t : P * t + P], rhs=ident[:],
                    is_transpose=True, start=False, stop=(b4 == 3),
                )
            nc.scalar.copy(
                out=ut[:, t, :, 4 * hb : 4 * hb + 4, :], in_=ob[:].rearrange("p b (h c) -> p h b c", h=2)
            )
            if hb == 1:
                nc.sync.dma_start(
                    out=oview[:, 2 * i : 2 * i + 2, t : t + 1, :].rearrange("p h o f -> p (h o) f"),
                    in_=ut[:, t].rearrange("p h b c -> p h (b c)"),
                )

        for be in range(4):
            xs = xss[be]
            xg = slot([P, 2, 512, 4], BF16, "xg", "C")
            xg32 = xg[:].bitcast(F32)
            for g in range(2):
                for bb in range(2):
                    xtag = ("tr", "ob", "ob", "mt")[2 * g + bb]
                    xt = ps.tile([P, 2, 2, P], F32, name="xt", tag=xtag, bufs=PSB[xtag])
                    for t in range(2):
                        xw = xs[:, t, bb, :].bitcast(F32)
                        for u in range(2):
                            w0 = 256 * g + 128 * u
                            nc.tensor.transpose(xt[:, t, u, :], xw[:, w0 : w0 + 128], ident[:])
                    dst = xg32[:, g, 256 * bb : 256 * bb + 256, :].rearrange("p (t k) u -> p t k u", t=2)
                    src = xt[:].rearrange("p t u k -> p t k u")
                    if g == 0 and bb == 0:
                        nc.vector.tensor_copy(out=dst, in_=src)
                    else:
                        nc.scalar.copy(out=dst, in_=src)
            if be >= 1:
                keys(0, be - 1, "kv"[be % 2])
            if be >= 2:
                mag_a(0, be - 2)
            for g in range(2):
                nc.vector.quantize_mx(
                    out=xc[:, g, 512 * be : 512 * be + 512].bitcast(FP8X4),
                    scales=xsc[:, g, 512 * be : 512 * be + 512],
                    in_=xg[:, g].rearrange("p c j -> p (c j)"),
                )
        keys(0, 3, "k")
        mag_a(0, 2)
        mag_a(0, 3)
        mag_b(0)
        mag_c(0)
        quant_w(wst_b, DM)
        values(0, 0)
        values(0, 1)
        for be in range(4):
            keys(1, be, ("k", "ob", "ob", "tr")[be])
        for be in range(4):
            mag_a(1, be)
        for be in range(4):
            keys(2, be, ("k", "ob", "ob", "tr")[be])
        mag_b(1)
        mag_c(1)

        CHAIN_ROUNDS = (((1, 0), (1, 1)), ((2, 0), (2, 1), (3, 0)), ((3, 1), (4, 0), (4, 1)), ((5, 0), (5, 1)))
        LAST_TAGS = ("v", "v", "k", "tr")

        def period(i):
            for r in range(4):
                t, hb = r // 2, r % 2
                if 0 <= i + 1 < 8 and (i >= 0 or r >= 2):
                    values(i + 1, r)
                if i == 0:
                    keys(3 + r // 2, 2 * (r % 2), "k")
                    keys(3 + r // 2, 2 * (r % 2) + 1, "ob")
                elif 5 <= i + 4 < 8:
                    keys(i + 4, r)
                if 0 <= i < 8:
                    field_to_tokens(i, t, hb)
                if 0 <= i - 1 < 7:
                    toeplitz(i - 1, t, hb, "ob")
                if 0 <= i - 1 < 8:
                    finish(i - 1, t, hb)
                if r == 3 and 3 <= i + 3 < 8:
                    mag_b(i + 3)
                if i == 0:
                    if r == 0 or r == 2:
                        for be in range(4):
                            mag_a(2 + r // 2, be)
                    if r == 1:
                        mag_b(2)
                        mag_c(2)
                if 4 <= i + 3 < 8 and r < 3:
                    mag_a(i + 3, r)
                    if r == 2:
                        mag_a(i + 3, 3)
                if 0 <= i < 8:
                    for tap, part in CHAIN_ROUNDS[r]:
                        chain(i, tap, part)
                if 0 <= i + 1 < 8:
                    field(i + 1, r)
                    first_tap(i + 1, r)
                if r == 3 and 3 <= i + 3 < 8:
                    mag_c(i + 3)
                if r == 3 and 0 <= i < 8:
                    skips(i)
            if i == 7:
                for r in range(4):
                    toeplitz(7, r // 2, r % 2, LAST_TAGS[r])

        fv = fp[:, 0 : NH * 384].rearrange("p (h y) -> p h y", y=384)
        big = [(0, t0[:])]
        big += [(2**m, pt[:, m + 3, :]) for m in range(8)]
        big += [(3 * 2**m, rt[:, m + 3, :]) for m in range(7)]
        for sig, src in big:
            for shift, scal in ((0, 1.0), (64, sw[:, 0:1]), (128, sw[:, 1:2])):
                if sig + shift < NQ:
                    pos = 128 + sig + shift
                    nc.vector.scalar_tensor_tensor(
                        out=fv[:, :, pos : pos + 1],
                        in0=src.unsqueeze(2),
                        scalar=scal,
                        in1=fv[:, :, pos : pos + 1],
                        op0=ALU.mult,
                        op1=ALU.add,
                    )
        nc.sync.dma_start(
            out=oflat[TOEP_BASE : TOEP_BASE + P * FROW].rearrange("(p f) -> p f", f=FROW), in_=fp[:]
        )
        nc.sync.dma_start(
            out=wt[:],
            in_=oflat[TOEP_BASE + 128 : TOEP_BASE + 128 + P * (FROW - 1)].rearrange(
                "(p h y) -> p h y", h=NH, y=384
            )[:, :, 0:NQ],
        )
        quant_w(wst_c, 512)
        quant_w(wst_d, DM + 512)
        for i in range(-1, 9):
            period(i)
